import numpy as np
import ml_dtypes


def mxq(x, axis, fmt="e4m3"):
    dtype, down = {"e4m3": (ml_dtypes.float8_e4m3fn, 7), "e5m2": (ml_dtypes.float8_e5m2, 14)}[fmt]
    v = np.moveaxis(np.asarray(x, np.float32).astype(ml_dtypes.bfloat16).astype(np.float64), axis, -1)
    blocks = v.reshape(v.shape[:-1] + (-1, 32))
    amax = np.abs(blocks).max(-1, keepdims=True)
    byte = np.maximum(np.where(amax > 0, np.frexp(amax)[1] - 1 + 127, 0) - down, 1)
    scale = np.exp2(byte - 127.0)
    codes = (blocks / scale).astype(np.float32).astype(dtype).astype(np.float64)
    return np.moveaxis((codes * scale).reshape(v.shape), -1, axis)


WIDE = False


def mx_kscale(k):
    if not WIDE:
        return np.ones(k)
    levels = np.array([10, -10, 5, -5, 0])
    if k % 512:
        return np.exp2(np.random.permutation(np.resize(levels, k // 32))).repeat(32)
    a = np.empty((k // 512, 16))
    for p in range(k // 512):
        a[p, :8] = np.random.permutation(np.resize(levels, 8))
        for g in range(8):
            far = levels[np.abs(levels - a[p, g]) >= 10]
            a[p, g + 8] = far[np.random.randint(len(far))]
    return np.exp2(a.ravel()).repeat(32)


BF16 = ml_dtypes.bfloat16


def bf(x):
    return np.asarray(x, np.float32).astype(BF16)


def f64(x):
    return np.asarray(x).astype(np.float64)


B, C, W, H, O = 4096, 64, 4, 4, 1024
K = C * W * H
G = np.sqrt(W * H)
SLO, SHI = 1.0 + 0.03 * G, 2.0 + 0.25 * G


def setup_inputs():
    t = mx_kscale(K).reshape(C, W * H)[np.arange(C), np.arange(C) * (W * H) // C].reshape(1, C, 1, 1)
    return {"x": bf(np.random.standard_normal((B, C, W, H)) * t),
            "cx": bf(np.random.uniform(-W / 2.0, W / 2.0, (O, 1, 1, 1))),
            "cy": bf(np.random.uniform(-H / 2.0, H / 2.0, (O, 1, 1, 1))),
            "sigma": bf(np.random.uniform(SLO, SHI, (O, 1, 1, 1))),
            "features": bf(np.random.standard_normal((O, C, 1, 1)) * 2.0 / (np.sqrt(C) * (SLO + SHI)) / t),
            "bias": bf(np.random.standard_normal(O))}


def reference(x, cx, cy, sigma, features, bias):
    x, cx, cy, sigma, features, bias = f64(x), f64(cx), f64(cy), f64(sigma), f64(features), f64(bias)
    w_edge = (W - 1) / 2.0
    h_edge = (H - 1) / 2.0
    grid_x = np.linspace(-w_edge, w_edge, W).reshape(1, 1, W, 1)
    grid_y = np.linspace(-h_edge, h_edge, H).reshape(1, 1, 1, H)
    d = (cx - grid_x) ** 2 + (cy - grid_y) ** 2
    spatial = np.exp(-d / sigma ** 2)
    weight = (spatial * features).reshape(O, K)
    return (mxq(x.reshape(B, K), 1, "e4m3") @ mxq(weight, 1, "e4m3").T) + bias

@@ -1,0 +1,327 @@
+from contextlib import ExitStack
+
+import concourse.mybir as mybir
+from concourse.masks import make_identity
+
+F32 = mybir.dt.float32
+BF16 = mybir.dt.bfloat16
+U32 = mybir.dt.uint32
+U8 = mybir.dt.uint8
+FP8X4 = mybir.dt.float8_e4m3fn_x4
+ALU = mybir.AluOpType
+ACT = mybir.ActivationFunctionType
+
+P = 128
+B, C, O, K = 4096, 64, 1024, 1024
+HALF = 512
+QUARTER = 256
+TILES = 4
+CHUNKS = B // (TILES * P)
+TRANSPOSE_BANKS = 3
+FLOPS = 2 * B * K * O
+
+
+def tile_gaussianspatialxfeaturelinear_t_kernel(tc, x, cx, cy, sigma, features, bias, out):
+    nc = tc.nc
+    with ExitStack() as ctx:
+        const = ctx.enter_context(tc.tile_pool(name="const", bufs=1))
+        xin = ctx.enter_context(tc.tile_pool(name="xin", bufs=1))
+        stage = ctx.enter_context(tc.tile_pool(name="stage", bufs=3))
+        outp = ctx.enter_context(tc.tile_pool(name="outp", bufs=6))
+        psum = ctx.enter_context(tc.psum_pool(name="psum", bufs=4))
+        ctx.enter_context(tc.manual_schedule())
+
+        x_chunks = x.rearrange("(n p r) c w h -> n p r (c w h)", p=P, r=TILES)
+        y_chunks = out.rearrange("(n p r) o -> n p r o", p=P, r=TILES)
+
+        def transpose_bank(shape, dtype, name):
+            return psum.tile(shape, dtype, name=name, tag="tp", bufs=TRANSPOSE_BANKS)
+
+        def matmul_bank(shape, dtype, name):
+            return psum.tile(shape, dtype, name=name, tag="acc", bufs=8 - TRANSPOSE_BANKS)
+
+        ident_b = const.tile([P, P], BF16, name="ident_b")
+        ident_f = const.tile([P, P], F32, name="ident_f")
+        make_identity(nc, ident_b[:])
+        make_identity(nc, ident_f[:])
+        vec_rows = const.tile([P, P], BF16, name="zrows")
+        nc.vector.memset(vec_rows[:], 0.0)
+        bias_row = const.tile([P, O], BF16, name="brow")
+        nc.vector.memset(bias_row[:], 0.0)
+        ones_b = const.tile([P, P], BF16, name="ones_b")
+        nc.vector.memset(ones_b[:], 1.0)
+        zero_col = const.tile([P, 1], F32, name="warm")
+        nc.vector.memset(zero_col[:], 0.0)
+        grid = const.tile([P, 4], F32, name="grid")
+        for i in range(4):
+            nc.vector.memset(grid[:, i : i + 1], i - 1.5)
+        select = const.tile([P, 4 * P], BF16, name="sel")
+        nc.vector.tensor_copy(
+            out=select[:].rearrange("p (r s) -> p r s", s=4),
+            in_=ident_b[:].unsqueeze(2).to_broadcast([P, P, 4]),
+        )
+
+        for n, vec in enumerate((cx, cy, sigma)):
+            nc.sync.dma_start(out=vec_rows[8 * n : 8 * n + 8, :], in_=vec.rearrange("(t p) a b c -> t (p a b c)", p=P))
+        nc.scalar.dma_start(out=bias_row[0:1, :], in_=bias.rearrange("(a o) -> a o", a=1))
+        feat = const.tile([P, 8, C], BF16, name="fsb")
+        x_raw = []
+        for n in range(CHUNKS):
+            x_tile = xin.tile([P, TILES, K], BF16, name="x%d" % n)
+            x_raw.append(x_tile)
+            if n == 0:
+                nc.sync.dma_start(out=x_tile[:, 0:2, :], in_=x_chunks[n][:, 0:2, :])
+                nc.sync.dma_start(out=feat[:], in_=features.rearrange("(t p) c a b -> p t (c a b)", p=P))
+                nc.sync.dma_start(out=x_tile[:, 2:4, :], in_=x_chunks[n][:, 2:4, :])
+            else:
+                nc.sync.dma_start(out=x_tile[:], in_=x_chunks[n])
+        one_col = const.tile([P, 1], F32, name="warm2")
+        nc.scalar.activation(out=one_col[:], in_=zero_col[:], func=ACT.Exp)
+
+        w_bf16 = const.tile([P, 2, O, 4], BF16, name="gw", align_bytes=64)
+        w_words = const.tile([P, 2, O], U32, name="wcod", align_bytes=64)
+        w_scales = const.tile([P, 2, O], U8, name="wscl", align_bytes=64)
+        x_words = [const.tile([P, TILES * 2 * P], U32, name="xcod%d" % n, align_bytes=64) for n in range(CHUNKS)]
+        x_scales = [const.tile([P, TILES * 2 * P], U8, name="xscl%d" % n, align_bytes=64) for n in range(CHUNKS)]
+        bias_all = const.tile([P, O], BF16, name="bias_sb")
+        spat_t = const.tile([P, 4, 4, QUARTER], F32, name="stsb")
+        feat_t = const.tile([P, 4 * P], BF16, name="ftsb")
+        x_bf16 = {}
+        x_banks = {}
+        y_pairs = {}
+
+        def transpose_x(n, r):
+            bank = transpose_bank([P, 4, P], F32, "tp")
+            words = x_raw[n][:, r, :].bitcast(F32)
+            for g in range(2):
+                for u in range(2):
+                    every_2nd = words[:, 2 * P * g + u : 2 * P * (g + 1) : 2]
+                    nc.tensor.transpose(bank[:, 2 * g + u, :], every_2nd, ident_f[:])
+            x_banks[(n, r)] = bank
+
+        def regroup_x(n, r, engine):
+            if n not in x_bf16:
+                x_bf16[n] = stage.tile([P, TILES, K], BF16, name="gx", align_bytes=64)
+            dst = x_bf16[n][:, r, :].bitcast(F32).rearrange("p (g b u) -> p g b u", g=2, u=2)
+            src = x_banks[(n, r)][:].rearrange("p (g u) b -> p g b u", g=2)
+            if engine == "scalar":
+                nc.scalar.copy(out=dst, in_=src)
+            else:
+                nc.vector.tensor_copy(out=dst, in_=src)
+
+        def stage_chunk(n):
+            for r in range(TILES):
+                transpose_x(n, r)
+            for r in range(TILES):
+                regroup_x(n, r, "scalar")
+
+        def quantise_x(n, first=0, count=TILES):
+            cols = slice(2 * P * first, 2 * P * (first + count))
+            nc.vector.quantize_mx(
+                out=x_words[n][:, cols].bitcast(FP8X4),
+                scales=x_scales[n][:, cols],
+                in_=x_bf16[n][:, first : first + count, :].rearrange("p r k -> p (r k)"),
+            )
+
+        def multiply(n, r, h, way_out):
+            if (n, r // 2) not in y_pairs:
+                y_pairs[(n, r // 2)] = outp.tile([P, 2, O], F32, name="osb")
+            half = slice(HALF * h, HALF * h + HALF)
+            bank = matmul_bank([P, HALF], F32, "acc")
+            for g in range(2):
+                cols = slice(2 * P * r + P * g, 2 * P * r + P * g + P)
+                nc.tensor.matmul_mx(
+                    out=bank[:],
+                    lhsT=x_words[n][:, cols].bitcast(FP8X4),
+                    lhsT_scale=x_scales[n][:, cols],
+                    rhs=w_words[:, g, half].bitcast(FP8X4),
+                    rhs_scale=w_scales[:, g, half],
+                    start=(g == 0),
+                    stop=(g == 1),
+                )
+            dst = y_pairs[(n, r // 2)][:, r % 2, half]
+            if way_out == "vector":
+                nc.vector.tensor_tensor(out=dst, in0=bank[:], in1=bias_all[:, half], op=ALU.add)
+            else:
+                nc.scalar.copy(out=dst, in_=bank[:])
+                nc.gpsimd.tensor_tensor(out=dst, in0=dst, in1=bias_all[:, half], op=ALU.add)
+
+        def store(n, first, count):
+            nc.sync.dma_start(
+                out=y_chunks[n][:, first : first + count, :],
+                in_=y_pairs[(n, first // 2)][:, first % 2 : first % 2 + count, :],
+            )
+
+        vec_bank = matmul_bank([P, P], BF16, "pz")
+        nc.tensor.transpose(vec_bank[:], vec_rows[:], ident_b[:])
+        vec_cols = const.tile([P, 24], F32, name="zt")
+        nc.vector.tensor_copy(out=vec_cols[:], in_=vec_bank[:, 0:24])
+        dist = const.tile([P, 2, 8, 4], F32, name="dxy")
+        nc.vector.tensor_tensor(
+            out=dist[:],
+            in0=vec_cols[:, 0:16].rearrange("p (a t) -> p a t", a=2).unsqueeze(3).to_broadcast([P, 2, 8, 4]),
+            in1=grid[:].unsqueeze(1).unsqueeze(1).to_broadcast([P, 2, 8, 4]),
+            op=ALU.subtract,
+        )
+        dist_sq = const.tile([P, 2, 8, 4], F32, name="sq")
+        nc.vector.tensor_tensor(out=dist_sq[:], in0=dist[:], in1=dist[:], op=ALU.mult)
+        sigma_sq = const.tile([P, 8], F32, name="s2")
+        nc.vector.tensor_tensor(out=sigma_sq[:], in0=vec_cols[:, 16:24], in1=vec_cols[:, 16:24], op=ALU.mult)
+        inv_sigma_sq = const.tile([P, 8], F32, name="rinv")
+        nc.vector.reciprocal(out=inv_sigma_sq[:], in_=sigma_sq[:])
+        dist_sum = const.tile([P, 8, 4, 4], F32, name="dd")
+        nc.vector.tensor_tensor(
+            out=dist_sum[:],
+            in0=dist_sq[:, 0, :, :].unsqueeze(2).to_broadcast([P, 8, 4, 4]),
+            in1=dist_sq[:, 1, :, :].unsqueeze(3).to_broadcast([P, 8, 4, 4]),
+            op=ALU.add,
+        )
+        exponent = const.tile([P, 8, 16], F32, name="qq")
+        nc.vector.tensor_tensor(
+            out=exponent[:],
+            in0=dist_sum[:].rearrange("p t j i -> p t (j i)"),
+            in1=inv_sigma_sq[:].unsqueeze(2).to_broadcast([P, 8, 16]),
+            op=ALU.mult,
+        )
+
+        def exp_repeated(q):
+            rep = stage.tile([P, 8, P], F32, name="sx", bufs=2)
+            nc.scalar.activation(
+                out=rep[:].rearrange("p b (s i) -> p b s i", i=4),
+                in_=exponent[:, 2 * q : 2 * q + 2, :]
+                .rearrange("p t (j i) -> p (t j) i", j=4)
+                .unsqueeze(2)
+                .to_broadcast([P, 8, 32, 4]),
+                func=ACT.Exp,
+                scale=-1.0,
+            )
+            return rep
+
+        def transpose_spat(rep):
+            banks = []
+            for a in range(2):
+                bank = transpose_bank([P, 4, P], F32, "pst")
+                for j in range(2):
+                    for t in range(2):
+                        nc.tensor.transpose(bank[:, 2 * j + t, :], rep[:, 4 * t + 2 * a + j, :], ident_f[:])
+                banks.append(bank)
+            return banks
+
+        def keep_spat(q, banks):
+            for a in range(2):
+                nc.scalar.copy(
+                    out=spat_t[:, q, 2 * a : 2 * a + 2, :],
+                    in_=banks[a][:].rearrange("p (j t) o -> p j (t o)", j=2),
+                )
+
+        def select_feat(g, q):
+            bank = matmul_bank([P, QUARTER], F32, "pft")
+            for s in range(2):
+                m = 2 * s + g
+                nc.tensor.matmul(
+                    out=bank[:, P * s : P * s + P],
+                    lhsT=select[:, P * m : P * m + P],
+                    rhs=feat_t[:, P * q : P * q + P],
+                    start=True,
+                    stop=True,
+                )
+            return bank
+
+        def build_w(g, q, feat_bank):
+            nc.vector.tensor_tensor(
+                out=w_bf16[:, g, QUARTER * q : QUARTER * q + QUARTER, :],
+                in0=feat_bank[:].unsqueeze(2).to_broadcast([P, QUARTER, 4]),
+                in1=spat_t[:, q, :, :].rearrange("p t o -> p o t"),
+                op=ALU.mult,
+            )
+
+        def quantise_w(g, h):
+            half = slice(HALF * h, HALF * h + HALF)
+            nc.vector.quantize_mx(
+                out=w_words[:, g, half].bitcast(FP8X4),
+                scales=w_scales[:, g, half],
+                in_=w_bf16[:, g, half, :].rearrange("p o t -> p (o t)"),
+            )
+
+        transpose_x(0, 0)
+        transpose_x(0, 1)
+        feat_bank_t = matmul_bank([P, 4, P], BF16, "pf")
+        for a in range(4):
+            nc.tensor.transpose(feat_bank_t[:, a, :], feat[:, 2 * a : 2 * a + 2, :].rearrange("p t c -> p (t c)"), ident_b[:])
+        rep0 = exp_repeated(0)
+        rep1 = exp_repeated(1)
+        regroup_x(0, 0, "vector")
+        nc.vector.tensor_copy(out=feat_t[:], in_=feat_bank_t[:].rearrange("p a o -> p (a o)"))
+        regroup_x(0, 1, "vector")
+        feat_banks = {}
+        keep_spat(0, transpose_spat(rep0))
+        feat_banks[(0, 0)] = select_feat(0, 0)
+        feat_banks[(1, 0)] = select_feat(1, 0)
+        spat_bank1 = transpose_spat(rep1)
+        rep2 = exp_repeated(2)
+        keep_spat(1, spat_bank1)
+        rep3 = exp_repeated(3)
+        quantise_x(0, 0, 2)
+        feat_banks[(0, 1)] = select_feat(0, 1)
+        feat_banks[(1, 1)] = select_feat(1, 1)
+        transpose_x(0, 2)
+        transpose_x(0, 3)
+        regroup_x(0, 2, "scalar")
+        regroup_x(0, 3, "scalar")
+        for q in range(2):
+            for g in range(2):
+                build_w(g, q, feat_banks[(g, q)])
+        keep_spat(2, transpose_spat(rep2))
+        keep_spat(3, transpose_spat(rep3))
+        bias_bank = transpose_bank([P, O], BF16, "pb")
+        for h in range(2):
+            half = slice(HALF * h, HALF * h + HALF)
+            nc.tensor.matmul(out=bias_bank[:, half], lhsT=ones_b[:], rhs=bias_row[:, half], start=True, stop=True)
+        nc.scalar.copy(out=bias_all[:], in_=bias_bank[:])
+        feat_banks[(0, 2)] = select_feat(0, 2)
+        feat_banks[(1, 2)] = select_feat(1, 2)
+        stage_chunk(1)
+        quantise_w(0, 0)
+        quantise_w(1, 0)
+
+        multiply(0, 0, 0, "scalar")
+        multiply(0, 1, 0, "scalar")
+        quantise_x(0, 2, 2)
+        multiply(0, 2, 0, "scalar")
+        multiply(0, 3, 0, "scalar")
+        build_w(0, 2, feat_banks[(0, 2)])
+        build_w(1, 2, feat_banks[(1, 2)])
+        feat_banks[(0, 3)] = select_feat(0, 3)
+        feat_banks[(1, 3)] = select_feat(1, 3)
+        stage_chunk(2)
+        quantise_x(1)
+        for r in range(TILES):
+            multiply(1, r, 0, "scalar")
+        build_w(0, 3, feat_banks[(0, 3)])
+        build_w(1, 3, feat_banks[(1, 3)])
+        quantise_w(0, 1)
+        quantise_w(1, 1)
+        quantise_x(2)
+        stage_chunk(3)
+
+        for n in range(2):
+            for r in range(TILES):
+                multiply(n, r, 1, "vector")
+                if r % 2 == 1:
+                    store(n, r - 1, 2)
+            if n == 0:
+                quantise_x(3)
+
+        for n in range(2, CHUNKS):
+            ahead = n + 2
+            if ahead < CHUNKS:
+                stage_chunk(ahead)
+            for r in range(TILES):
+                for h in range(2):
+                    if (r, h) == (2, 1) and ahead < CHUNKS:
+                        quantise_x(ahead)
+                    multiply(n, r, h, "scalar" if (r % 2, h) == (0, 0) else "vector")
+                if n == CHUNKS - 1:
+                    store(n, r, 1)
+                elif r % 2 == 1:
+                    store(n, r - 1, 2)

@@ -44,78 +44,83 @@ def tile_gaussianspatialxfeaturelinear_t_kernel(tc, x, cx, cy, sigma, features, 
         ident_f = const.tile([P, P], F32, name="ident_f")
         make_identity(nc, ident_b[:])
         make_identity(nc, ident_f[:])
-        vec_rows = const.tile([P, P], BF16, name="zrows")
+        vec_rows = const.tile([P, P], BF16, name="vec_rows")
         nc.vector.memset(vec_rows[:], 0.0)
-        bias_row = const.tile([P, O], BF16, name="brow")
-        nc.vector.memset(bias_row[:], 0.0)
-        ones_b = const.tile([P, P], BF16, name="ones_b")
-        nc.vector.memset(ones_b[:], 1.0)
-        zero_col = const.tile([P, 1], F32, name="warm")
+        zero_col = const.tile([P, 1], F32, name="zero_col")
         nc.vector.memset(zero_col[:], 0.0)
         grid = const.tile([P, 4], F32, name="grid")
         for i in range(4):
             nc.vector.memset(grid[:, i : i + 1], i - 1.5)
-        select = const.tile([P, 4 * P], BF16, name="sel")
-        nc.vector.tensor_copy(
-            out=select[:].rearrange("p (r s) -> p r s", s=4),
-            in_=ident_b[:].unsqueeze(2).to_broadcast([P, P, 4]),
-        )
+        bias_row = const.tile([P, O], BF16, name="bias_row")
+        nc.vector.memset(bias_row[:], 0.0)
+        ones_b = const.tile([P, P], BF16, name="ones_b")
+        nc.vector.memset(ones_b[:], 1.0)
 
         for n, vec in enumerate((cx, cy, sigma)):
             nc.sync.dma_start(out=vec_rows[8 * n : 8 * n + 8, :], in_=vec.rearrange("(t p) a b c -> t (p a b c)", p=P))
-        nc.scalar.dma_start(out=bias_row[0:1, :], in_=bias.rearrange("(a o) -> a o", a=1))
-        feat = const.tile([P, 8, C], BF16, name="fsb")
+        nc.sync.dma_start(out=bias_row[0:1, :], in_=bias.rearrange("(a o) -> a o", a=1))
+        feat = const.tile([P, 8, C], BF16, name="feat")
+        nc.sync.dma_start(out=feat[:], in_=features.rearrange("(t p) c a b -> p t (c a b)", p=P))
         x_raw = []
         for n in range(CHUNKS):
             x_tile = xin.tile([P, TILES, K], BF16, name="x%d" % n)
             x_raw.append(x_tile)
-            if n == 0:
-                nc.sync.dma_start(out=x_tile[:, 0:2, :], in_=x_chunks[n][:, 0:2, :])
-                nc.sync.dma_start(out=feat[:], in_=features.rearrange("(t p) c a b -> p t (c a b)", p=P))
-                nc.sync.dma_start(out=x_tile[:, 2:4, :], in_=x_chunks[n][:, 2:4, :])
+            if n < 2:
+                for r in (0, 2):
+                    nc.sync.dma_start(out=x_tile[:, r : r + 2, :], in_=x_chunks[n][:, r : r + 2, :])
             else:
                 nc.sync.dma_start(out=x_tile[:], in_=x_chunks[n])
-        one_col = const.tile([P, 1], F32, name="warm2")
+        one_col = const.tile([P, 1], F32, name="one_col")
         nc.scalar.activation(out=one_col[:], in_=zero_col[:], func=ACT.Exp)
 
-        w_bf16 = const.tile([P, 2, O, 4], BF16, name="gw", align_bytes=64)
-        w_words = const.tile([P, 2, O], U32, name="wcod", align_bytes=64)
-        w_scales = const.tile([P, 2, O], U8, name="wscl", align_bytes=64)
-        x_words = [const.tile([P, TILES * 2 * P], U32, name="xcod%d" % n, align_bytes=64) for n in range(CHUNKS)]
-        x_scales = [const.tile([P, TILES * 2 * P], U8, name="xscl%d" % n, align_bytes=64) for n in range(CHUNKS)]
-        bias_all = const.tile([P, O], BF16, name="bias_sb")
-        spat_t = const.tile([P, 4, 4, QUARTER], F32, name="stsb")
-        feat_t = const.tile([P, 4 * P], BF16, name="ftsb")
+        w_rows = const.tile([P, 8, K], BF16, name="w_rows")
+        w_bf16 = const.tile([P, 2, O, 4], BF16, name="w_bf16", align_bytes=64)
+        w_words = const.tile([P, 2, O], U32, name="w_words", align_bytes=64)
+        w_scales = const.tile([P, 2, O], U8, name="w_scales", align_bytes=64)
+        x_words = {}
+        x_scales = {}
+        bias_all = const.tile([P, O], BF16, name="bias_all")
+        x_perm = {}
         x_bf16 = {}
-        x_banks = {}
+        banks = {}
         y_pairs = {}
 
-        def transpose_x(n, r):
-            bank = transpose_bank([P, 4, P], F32, "tp")
-            words = x_raw[n][:, r, :].bitcast(F32)
-            for g in range(2):
-                for u in range(2):
-                    every_2nd = words[:, 2 * P * g + u : 2 * P * (g + 1) : 2]
-                    nc.tensor.transpose(bank[:, 2 * g + u, :], every_2nd, ident_f[:])
-            x_banks[(n, r)] = bank
-
-        def regroup_x(n, r, engine):
-            if n not in x_bf16:
-                x_bf16[n] = stage.tile([P, TILES, K], BF16, name="gx", align_bytes=64)
-            dst = x_bf16[n][:, r, :].bitcast(F32).rearrange("p (g b u) -> p g b u", g=2, u=2)
-            src = x_banks[(n, r)][:].rearrange("p (g u) b -> p g b u", g=2)
+        def permute_x(n, first, count, engine):
+            if n not in x_perm:
+                x_perm[n] = stage.tile([P, TILES, K], BF16, name="xp", bufs=2)
+            dst = x_perm[n][:, first : first + count, :].bitcast(F32).rearrange("p r (u w) -> p r u w", u=2)
+            src = x_raw[n][:, first : first + count, :].bitcast(F32).rearrange("p r (w u) -> p r u w", u=2)
             if engine == "scalar":
                 nc.scalar.copy(out=dst, in_=src)
             else:
                 nc.vector.tensor_copy(out=dst, in_=src)
 
-        def stage_chunk(n):
-            for r in range(TILES):
-                transpose_x(n, r)
-            for r in range(TILES):
-                regroup_x(n, r, "scalar")
+        def transpose_x(n, r):
+            bank = transpose_bank([P, 4, P], F32, "tp")
+            for g in range(2):
+                for u in range(2):
+                    if n in x_perm:
+                        first = 2 * P * u + P * g
+                        words = x_perm[n][:, r, :].bitcast(F32)[:, first : first + P]
+                    else:
+                        words = x_raw[n][:, r, :].bitcast(F32)[:, 2 * P * g + u : 2 * P * (g + 1) : 2]
+                    nc.tensor.transpose(bank[:, 2 * g + u, :], words, ident_f[:])
+            banks[(n, r)] = bank
+
+        def regroup_x(n, r, engine="scalar"):
+            if n not in x_bf16:
+                x_bf16[n] = stage.tile([P, TILES, K], BF16, name="gx", align_bytes=64)
+            dst = x_bf16[n][:, r, :].bitcast(F32).rearrange("p (g b u) -> p g b u", g=2, u=2)
+            src = banks[(n, r)][:].rearrange("p (g u) b -> p g b u", g=2)
+            if engine == "scalar":
+                nc.scalar.copy(out=dst, in_=src)
+            else:
+                nc.vector.tensor_copy(out=dst, in_=src)
 
         def quantise_x(n, first=0, count=TILES):
+            if n not in x_words:
+                x_words[n] = stage.tile([P, TILES * 2 * P], U32, name="x_words", bufs=4, align_bytes=64)
+                x_scales[n] = stage.tile([P, TILES * 2 * P], U8, name="x_scales", bufs=4, align_bytes=64)
             cols = slice(2 * P * first, 2 * P * (first + count))
             nc.vector.quantize_mx(
                 out=x_words[n][:, cols].bitcast(FP8X4),
@@ -125,7 +130,7 @@ def tile_gaussianspatialxfeaturelinear_t_kernel(tc, x, cx, cy, sigma, features, 
 
         def multiply(n, r, h, way_out):
             if (n, r // 2) not in y_pairs:
-                y_pairs[(n, r // 2)] = outp.tile([P, 2, O], F32, name="osb")
+                y_pairs[(n, r // 2)] = outp.tile([P, 2, O], F32, name="y_pair")
             half = slice(HALF * h, HALF * h + HALF)
             bank = matmul_bank([P, HALF], F32, "acc")
             for g in range(2):
@@ -152,176 +157,150 @@ def tile_gaussianspatialxfeaturelinear_t_kernel(tc, x, cx, cy, sigma, features, 
                 in_=y_pairs[(n, first // 2)][:, first % 2 : first % 2 + count, :],
             )
 
-        vec_bank = matmul_bank([P, P], BF16, "pz")
+        def store_half(n, r, h):
+            half = slice(HALF * h, HALF * h + HALF)
+            nc.sync.dma_start(out=y_chunks[n][:, r, half], in_=y_pairs[(n, r // 2)][:, r % 2, half])
+
+        vec_bank = matmul_bank([P, P], BF16, "vec_bank")
         nc.tensor.transpose(vec_bank[:], vec_rows[:], ident_b[:])
-        vec_cols = const.tile([P, 24], F32, name="zt")
-        nc.vector.tensor_copy(out=vec_cols[:], in_=vec_bank[:, 0:24])
-        dist = const.tile([P, 2, 8, 4], F32, name="dxy")
+        dist = const.tile([P, 2, 8, 4], F32, name="dist")
         nc.vector.tensor_tensor(
             out=dist[:],
-            in0=vec_cols[:, 0:16].rearrange("p (a t) -> p a t", a=2).unsqueeze(3).to_broadcast([P, 2, 8, 4]),
+            in0=vec_bank[:, 0:16].rearrange("p (a t) -> p a t", a=2).unsqueeze(3).to_broadcast([P, 2, 8, 4]),
             in1=grid[:].unsqueeze(1).unsqueeze(1).to_broadcast([P, 2, 8, 4]),
             op=ALU.subtract,
         )
-        dist_sq = const.tile([P, 2, 8, 4], F32, name="sq")
+        sigma_col = const.tile([P, 8], F32, name="sigma_col")
+        nc.vector.tensor_copy(out=sigma_col[:], in_=vec_bank[:, 16:24])
+        dist_sq = const.tile([P, 2, 8, 4], F32, name="dist_sq")
         nc.vector.tensor_tensor(out=dist_sq[:], in0=dist[:], in1=dist[:], op=ALU.mult)
-        sigma_sq = const.tile([P, 8], F32, name="s2")
-        nc.vector.tensor_tensor(out=sigma_sq[:], in0=vec_cols[:, 16:24], in1=vec_cols[:, 16:24], op=ALU.mult)
-        inv_sigma_sq = const.tile([P, 8], F32, name="rinv")
-        nc.vector.reciprocal(out=inv_sigma_sq[:], in_=sigma_sq[:])
-        dist_sum = const.tile([P, 8, 4, 4], F32, name="dd")
-        nc.vector.tensor_tensor(
-            out=dist_sum[:],
-            in0=dist_sq[:, 0, :, :].unsqueeze(2).to_broadcast([P, 8, 4, 4]),
-            in1=dist_sq[:, 1, :, :].unsqueeze(3).to_broadcast([P, 8, 4, 4]),
-            op=ALU.add,
+        neg_sigma_sq = const.tile([P, 8], F32, name="neg_sigma_sq")
+        nc.vector.scalar_tensor_tensor(
+            out=neg_sigma_sq[:], in0=sigma_col[:], scalar=-1.0, in1=sigma_col[:], op0=ALU.mult, op1=ALU.mult
         )
-        exponent = const.tile([P, 8, 16], F32, name="qq")
-        nc.vector.tensor_tensor(
-            out=exponent[:],
-            in0=dist_sum[:].rearrange("p t j i -> p t (j i)"),
-            in1=inv_sigma_sq[:].unsqueeze(2).to_broadcast([P, 8, 16]),
-            op=ALU.mult,
-        )
-
-        def exp_repeated(q):
-            rep = stage.tile([P, 8, P], F32, name="sx", bufs=2)
-            nc.scalar.activation(
-                out=rep[:].rearrange("p b (s i) -> p b s i", i=4),
-                in_=exponent[:, 2 * q : 2 * q + 2, :]
-                .rearrange("p t (j i) -> p (t j) i", j=4)
-                .unsqueeze(2)
-                .to_broadcast([P, 8, 32, 4]),
-                func=ACT.Exp,
-                scale=-1.0,
-            )
-            return rep
-
-        def transpose_spat(rep):
-            banks = []
-            for a in range(2):
-                bank = transpose_bank([P, 4, P], F32, "pst")
-                for j in range(2):
-                    for t in range(2):
-                        nc.tensor.transpose(bank[:, 2 * j + t, :], rep[:, 4 * t + 2 * a + j, :], ident_f[:])
-                banks.append(bank)
-            return banks
-
-        def keep_spat(q, banks):
-            for a in range(2):
-                nc.scalar.copy(
-                    out=spat_t[:, q, 2 * a : 2 * a + 2, :],
-                    in_=banks[a][:].rearrange("p (j t) o -> p j (t o)", j=2),
-                )
-
-        def select_feat(g, q):
-            bank = matmul_bank([P, QUARTER], F32, "pft")
-            for s in range(2):
-                m = 2 * s + g
-                nc.tensor.matmul(
-                    out=bank[:, P * s : P * s + P],
-                    lhsT=select[:, P * m : P * m + P],
-                    rhs=feat_t[:, P * q : P * q + P],
-                    start=True,
-                    stop=True,
-                )
-            return bank
-
-        def build_w(g, q, feat_bank):
+        dist_sum = const.tile([P, 8, 2, 4, 2], F32, name="dist_sum")
+        exp_scale = const.tile([P, 8], F32, name="exp_scale")
+        for u in range(2):
             nc.vector.tensor_tensor(
-                out=w_bf16[:, g, QUARTER * q : QUARTER * q + QUARTER, :],
-                in0=feat_bank[:].unsqueeze(2).to_broadcast([P, QUARTER, 4]),
-                in1=spat_t[:, q, :, :].rearrange("p t o -> p o t"),
-                op=ALU.mult,
+                out=dist_sum[:, :, u, :, :],
+                in0=dist_sq[:, 0, :, :].unsqueeze(3).to_broadcast([P, 8, 4, 2]),
+                in1=dist_sq[:, 1, :, 2 * u : 2 * u + 2].unsqueeze(2).to_broadcast([P, 8, 4, 2]),
+                op=ALU.add,
             )
+            if u == 0:
+                nc.vector.reciprocal(out=exp_scale[:], in_=neg_sigma_sq[:])
+        spat = const.tile([P, 8, 2, 8], F32, name="spat")
+        feat_bank = matmul_bank([P, 8, C], F32, "feat_bank")
 
-        def quantise_w(g, h):
-            half = slice(HALF * h, HALF * h + HALF)
-            nc.vector.quantize_mx(
-                out=w_words[:, g, half].bitcast(FP8X4),
-                scales=w_scales[:, g, half],
-                in_=w_bf16[:, g, half, :].rearrange("p o t -> p (o t)"),
-            )
+        def build_w(t, engine):
+            shape = [P, 2, C, 8]
+            in1 = spat[:, t, :, :].unsqueeze(2).to_broadcast(shape)
+            dst = w_rows[:, t, :].rearrange("p (u c m) -> p u c m", u=2, c=C)
+            if engine == "vector":
+                in0 = feat_bank[:, t, :].unsqueeze(1).unsqueeze(3).to_broadcast(shape)
+                nc.vector.tensor_tensor(out=dst, in0=in0, in1=in1, op=ALU.mult)
+            else:
+                in0 = feat[:, t, :].unsqueeze(1).unsqueeze(3).to_broadcast(shape)
+                nc.gpsimd.tensor_tensor(out=dst, in0=in0, in1=in1, op=ALU.mult)
 
-        transpose_x(0, 0)
-        transpose_x(0, 1)
-        feat_bank_t = matmul_bank([P, 4, P], BF16, "pf")
-        for a in range(4):
-            nc.tensor.transpose(feat_bank_t[:, a, :], feat[:, 2 * a : 2 * a + 2, :].rearrange("p t c -> p (t c)"), ident_b[:])
-        rep0 = exp_repeated(0)
-        rep1 = exp_repeated(1)
-        regroup_x(0, 0, "vector")
-        nc.vector.tensor_copy(out=feat_t[:], in_=feat_bank_t[:].rearrange("p a o -> p (a o)"))
-        regroup_x(0, 1, "vector")
-        feat_banks = {}
-        keep_spat(0, transpose_spat(rep0))
-        feat_banks[(0, 0)] = select_feat(0, 0)
-        feat_banks[(1, 0)] = select_feat(1, 0)
-        spat_bank1 = transpose_spat(rep1)
-        rep2 = exp_repeated(2)
-        keep_spat(1, spat_bank1)
-        rep3 = exp_repeated(3)
-        quantise_x(0, 0, 2)
-        feat_banks[(0, 1)] = select_feat(0, 1)
-        feat_banks[(1, 1)] = select_feat(1, 1)
-        transpose_x(0, 2)
-        transpose_x(0, 3)
-        regroup_x(0, 2, "scalar")
-        regroup_x(0, 3, "scalar")
-        for q in range(2):
+        def transpose_w(t):
+            bank = transpose_bank([P, 4, P], F32, "tp")
             for g in range(2):
-                build_w(g, q, feat_banks[(g, q)])
-        keep_spat(2, transpose_spat(rep2))
-        keep_spat(3, transpose_spat(rep3))
-        bias_bank = transpose_bank([P, O], BF16, "pb")
+                for u in range(2):
+                    first = 2 * P * u + P * g
+                    nc.tensor.transpose(bank[:, 2 * g + u, :], w_rows[:, t, :].bitcast(F32)[:, first : first + P], ident_f[:])
+            nc.scalar.copy(
+                out=w_bf16[:, :, P * t : P * t + P, :].rearrange("p g o k -> p g (o k)").bitcast(F32).rearrange("p g (o u) -> p g o u", u=2),
+                in_=bank[:].rearrange("p (g u) b -> p g b u", g=2),
+            )
+
+        def quantise_w(q):
+            cols = slice(QUARTER * q, QUARTER * q + QUARTER)
+            for g in range(2):
+                nc.vector.quantize_mx(
+                    out=w_words[:, g, cols].bitcast(FP8X4),
+                    scales=w_scales[:, g, cols],
+                    in_=w_bf16[:, g, cols, :].rearrange("p o t -> p (o t)"),
+                )
+
+        nc.tensor.matmul(out=feat_bank[:].rearrange("p t c -> p (t c)"), lhsT=ident_b[:], rhs=feat[:].rearrange("p t c -> p (t c)"), start=True, stop=True)
+        bias_bank = matmul_bank([P, O], BF16, "bias_bank")
         for h in range(2):
             half = slice(HALF * h, HALF * h + HALF)
             nc.tensor.matmul(out=bias_bank[:, half], lhsT=ones_b[:], rhs=bias_row[:, half], start=True, stop=True)
-        nc.scalar.copy(out=bias_all[:], in_=bias_bank[:])
-        feat_banks[(0, 2)] = select_feat(0, 2)
-        feat_banks[(1, 2)] = select_feat(1, 2)
-        stage_chunk(1)
-        quantise_w(0, 0)
-        quantise_w(1, 0)
-
+        for t in (0, 3, 1, 2, 7, 6, 4, 5):
+            nc.scalar.activation(
+                out=spat[:, t, :, :].rearrange("p u m -> p (u m)"),
+                in_=dist_sum[:, t, :, :, :].rearrange("p u i e -> p (u i e)"),
+                func=ACT.Exp,
+                scale=exp_scale[:, t : t + 1],
+            )
+        transpose_x(0, 0)
+        regroup_x(0, 0)
+        transpose_x(0, 1)
+        regroup_x(0, 1)
+        build_w(0, "vector")
+        build_w(3, "gpsimd")
+        build_w(1, "vector")
+        build_w(7, "gpsimd")
+        transpose_w(0)
+        transpose_x(0, 2)
+        regroup_x(0, 2)
+        build_w(2, "vector")
+        nc.vector.tensor_copy(out=bias_all[:], in_=bias_bank[:])
+        transpose_w(1)
+        transpose_w(3)
+        build_w(6, "gpsimd")
+        quantise_w(0)
+        quantise_x(0, 0, 2)
+        transpose_w(2)
+        transpose_x(0, 3)
+        regroup_x(0, 3)
+        quantise_w(1)
+        transpose_w(7)
+        transpose_x(1, 0)
+        regroup_x(1, 0)
+        build_w(4, "vector")
         multiply(0, 0, 0, "scalar")
         multiply(0, 1, 0, "scalar")
         quantise_x(0, 2, 2)
+        build_w(5, "vector")
+        transpose_w(6)
+        transpose_w(4)
         multiply(0, 2, 0, "scalar")
         multiply(0, 3, 0, "scalar")
-        build_w(0, 2, feat_banks[(0, 2)])
-        build_w(1, 2, feat_banks[(1, 2)])
-        feat_banks[(0, 3)] = select_feat(0, 3)
-        feat_banks[(1, 3)] = select_feat(1, 3)
-        stage_chunk(2)
-        quantise_x(1)
+        transpose_w(5)
+        quantise_w(3)
+        permute_x(2, 0, 4, "vector")
+        quantise_w(2)
+        quantise_x(1, 0, 1)
+        for r in range(1, TILES):
+            transpose_x(1, r)
         for r in range(TILES):
-            multiply(1, r, 0, "scalar")
-        build_w(0, 3, feat_banks[(0, 3)])
-        build_w(1, 3, feat_banks[(1, 3)])
-        quantise_w(0, 1)
-        quantise_w(1, 1)
-        quantise_x(2)
-        stage_chunk(3)
+            multiply(0, r, 1, "scalar" if r == 0 else "vector")
+            if r > 0:
+                regroup_x(1, r)
+            store(0, r, 1)
+        quantise_x(1, 1, 1)
+        quantise_x(1, 2, 2)
 
-        for n in range(2):
-            for r in range(TILES):
-                multiply(n, r, 1, "vector")
-                if r % 2 == 1:
-                    store(n, r - 1, 2)
-            if n == 0:
-                quantise_x(3)
-
-        for n in range(2, CHUNKS):
-            ahead = n + 2
+        for n in range(1, CHUNKS):
+            ahead = n + 1
             if ahead < CHUNKS:
-                stage_chunk(ahead)
+                for r in range(TILES):
+                    transpose_x(ahead, r)
+                for r in range(TILES):
+                    regroup_x(ahead, r)
+            if n + 2 < CHUNKS:
+                permute_x(n + 2, 0, 2, "vector")
             for r in range(TILES):
                 for h in range(2):
-                    if (r, h) == (2, 1) and ahead < CHUNKS:
-                        quantise_x(ahead)
-                    multiply(n, r, h, "scalar" if (r % 2, h) == (0, 0) else "vector")
-                if n == CHUNKS - 1:
+                    if ahead < CHUNKS and h == 1 and r in (1, 2):
+                        quantise_x(ahead, 2 * (r - 1), 2)
+                    multiply(n, r, h, "scalar" if (r, h) in ((1, 0), (2, 1)) else "vector")
+                    if n + 2 < CHUNKS and (r, h) == (1, 0):
+                        permute_x(n + 2, 2, 2, "scalar")
+                    if (n, r) == (CHUNKS - 1, TILES - 1):
+                        store_half(n, r, h)
+                if (n, r) != (CHUNKS - 1, TILES - 1):
                     store(n, r, 1)
-                elif r % 2 == 1:
-                    store(n, r - 1, 2)

@@ -192,16 +192,12 @@ def tile_gaussianspatialxfeaturelinear_t_kernel(tc, x, cx, cy, sigma, features, 
         spat = const.tile([P, 8, 2, 8], F32, name="spat")
         feat_bank = matmul_bank([P, 8, C], F32, "feat_bank")
 
-        def build_w(t, engine):
+        def build_w(t):
             shape = [P, 2, C, 8]
             in1 = spat[:, t, :, :].unsqueeze(2).to_broadcast(shape)
             dst = w_rows[:, t, :].rearrange("p (u c m) -> p u c m", u=2, c=C)
-            if engine == "vector":
-                in0 = feat_bank[:, t, :].unsqueeze(1).unsqueeze(3).to_broadcast(shape)
-                nc.vector.tensor_tensor(out=dst, in0=in0, in1=in1, op=ALU.mult)
-            else:
-                in0 = feat[:, t, :].unsqueeze(1).unsqueeze(3).to_broadcast(shape)
-                nc.gpsimd.tensor_tensor(out=dst, in0=in0, in1=in1, op=ALU.mult)
+            in0 = feat_bank[:, t, :].unsqueeze(1).unsqueeze(3).to_broadcast(shape)
+            nc.vector.tensor_tensor(out=dst, in0=in0, in1=in1, op=ALU.mult)
 
         def transpose_w(t):
             bank = transpose_bank([P, 4, P], F32, "tp")
@@ -228,7 +224,7 @@ def tile_gaussianspatialxfeaturelinear_t_kernel(tc, x, cx, cy, sigma, features, 
         for h in range(2):
             half = slice(HALF * h, HALF * h + HALF)
             nc.tensor.matmul(out=bias_bank[:, half], lhsT=ones_b[:], rhs=bias_row[:, half], start=True, stop=True)
-        for t in (0, 3, 1, 2, 7, 6, 4, 5):
+        for t in range(8):
             nc.scalar.activation(
                 out=spat[:, t, :, :].rearrange("p u m -> p (u m)"),
                 in_=dist_sum[:, t, :, :, :].rearrange("p u i e -> p (u i e)"),
@@ -239,40 +235,40 @@ def tile_gaussianspatialxfeaturelinear_t_kernel(tc, x, cx, cy, sigma, features, 
         regroup_x(0, 0)
         transpose_x(0, 1)
         regroup_x(0, 1)
-        build_w(0, "vector")
-        build_w(3, "gpsimd")
-        build_w(1, "vector")
-        build_w(7, "gpsimd")
+        build_w(0)
+        build_w(1)
         transpose_w(0)
         transpose_x(0, 2)
         regroup_x(0, 2)
-        build_w(2, "vector")
+        build_w(2)
+        build_w(3)
         nc.vector.tensor_copy(out=bias_all[:], in_=bias_bank[:])
         transpose_w(1)
-        transpose_w(3)
-        build_w(6, "gpsimd")
         quantise_w(0)
         quantise_x(0, 0, 2)
         transpose_w(2)
         transpose_x(0, 3)
         regroup_x(0, 3)
+        transpose_w(3)
         quantise_w(1)
-        transpose_w(7)
         transpose_x(1, 0)
         regroup_x(1, 0)
-        build_w(4, "vector")
+        build_w(4)
+        build_w(5)
         multiply(0, 0, 0, "scalar")
         multiply(0, 1, 0, "scalar")
         quantise_x(0, 2, 2)
-        build_w(5, "vector")
-        transpose_w(6)
+        build_w(6)
         transpose_w(4)
+        transpose_w(5)
         multiply(0, 2, 0, "scalar")
         multiply(0, 3, 0, "scalar")
-        transpose_w(5)
-        quantise_w(3)
-        permute_x(2, 0, 4, "vector")
+        build_w(7)
         quantise_w(2)
+        transpose_w(6)
+        transpose_w(7)
+        permute_x(2, 0, 4, "vector")
+        quantise_w(3)
         quantise_x(1, 0, 1)
         for r in range(1, TILES):
             transpose_x(1, r)

@@ -288,14 +288,12 @@ def tile_gaussianspatialxfeaturelinear_t_kernel(tc, x, cx, cy, sigma, features, 
                 for r in range(TILES):
                     regroup_x(ahead, r)
             if n + 2 < CHUNKS:
-                permute_x(n + 2, 0, 2, "vector")
+                permute_x(n + 2, 0, 4, "scalar")
             for r in range(TILES):
                 for h in range(2):
                     if ahead < CHUNKS and h == 1 and r in (1, 2):
                         quantise_x(ahead, 2 * (r - 1), 2)
-                    multiply(n, r, h, "scalar" if (r, h) in ((1, 0), (2, 1)) else "vector")
-                    if n + 2 < CHUNKS and (r, h) == (1, 0):
-                        permute_x(n + 2, 2, 2, "scalar")
+                    multiply(n, r, h, "vector")
                     if (n, r) == (CHUNKS - 1, TILES - 1):
                         store_half(n, r, h)
                 if (n, r) != (CHUNKS - 1, TILES - 1):

@@ -17,6 +17,7 @@ HALF = 512
 QUARTER = 256
 TILES = 4
 CHUNKS = B // (TILES * P)
+PAIRS = B // (2 * P)
 TRANSPOSE_BANKS = 3
 FLOPS = 2 * B * K * O
 
@@ -80,30 +81,15 @@ def tile_gaussianspatialxfeaturelinear_t_kernel(tc, x, cx, cy, sigma, features, 
         x_words = {}
         x_scales = {}
         bias_all = const.tile([P, O], BF16, name="bias_all")
-        x_perm = {}
         x_bf16 = {}
         banks = {}
         y_pairs = {}
-
-        def permute_x(n, first, count, engine):
-            if n not in x_perm:
-                x_perm[n] = stage.tile([P, TILES, K], BF16, name="xp", bufs=2)
-            dst = x_perm[n][:, first : first + count, :].bitcast(F32).rearrange("p r (u w) -> p r u w", u=2)
-            src = x_raw[n][:, first : first + count, :].bitcast(F32).rearrange("p r (w u) -> p r u w", u=2)
-            if engine == "scalar":
-                nc.scalar.copy(out=dst, in_=src)
-            else:
-                nc.vector.tensor_copy(out=dst, in_=src)
 
         def transpose_x(n, r):
             bank = transpose_bank([P, 4, P], F32, "tp")
             for g in range(2):
                 for u in range(2):
-                    if n in x_perm:
-                        first = 2 * P * u + P * g
-                        words = x_perm[n][:, r, :].bitcast(F32)[:, first : first + P]
-                    else:
-                        words = x_raw[n][:, r, :].bitcast(F32)[:, 2 * P * g + u : 2 * P * (g + 1) : 2]
+                    words = x_raw[n][:, r, :].bitcast(F32)[:, 2 * P * g + u : 2 * P * (g + 1) : 2]
                     nc.tensor.transpose(bank[:, 2 * g + u, :], words, ident_f[:])
             banks[(n, r)] = bank
 
@@ -116,6 +102,13 @@ def tile_gaussianspatialxfeaturelinear_t_kernel(tc, x, cx, cy, sigma, features, 
                 nc.scalar.copy(out=dst, in_=src)
             else:
                 nc.vector.tensor_copy(out=dst, in_=src)
+
+        def stage_pair(pair):
+            n, first = divmod(pair, 2)
+            for r in (2 * first, 2 * first + 1):
+                transpose_x(n, r)
+            for r in (2 * first, 2 * first + 1):
+                regroup_x(n, r)
 
         def quantise_x(n, first=0, count=TILES):
             if n not in x_words:
@@ -149,7 +142,13 @@ def tile_gaussianspatialxfeaturelinear_t_kernel(tc, x, cx, cy, sigma, features, 
                 nc.vector.tensor_tensor(out=dst, in0=bank[:], in1=bias_all[:, half], op=ALU.add)
             else:
                 nc.scalar.copy(out=dst, in_=bank[:])
-                nc.gpsimd.tensor_tensor(out=dst, in0=dst, in1=bias_all[:, half], op=ALU.add)
+                if way_out == "scalar":
+                    add_bias(n, r, h)
+
+        def add_bias(n, r, h):
+            half = slice(HALF * h, HALF * h + HALF)
+            dst = y_pairs[(n, r // 2)][:, r % 2, half]
+            nc.gpsimd.tensor_tensor(out=dst, in0=dst, in1=bias_all[:, half], op=ALU.add)
 
         def store(n, first, count):
             nc.sync.dma_start(
@@ -161,8 +160,17 @@ def tile_gaussianspatialxfeaturelinear_t_kernel(tc, x, cx, cy, sigma, features, 
             half = slice(HALF * h, HALF * h + HALF)
             nc.sync.dma_start(out=y_chunks[n][:, r, half], in_=y_pairs[(n, r // 2)][:, r % 2, half])
 
+        def keep_warm(count):
+            for i in range(count):
+                nc.tensor.matmul(out=warm_bank[:], lhsT=ones_b[:], rhs=warm_cols[:], start=True, stop=True)
+
+        warm_cols = const.tile([P, HALF], BF16, name="warm_cols")
+        nc.gpsimd.memset(warm_cols[:], 0.0)
+        warm_bank = matmul_bank([P, HALF], F32, "warm_bank")
+        keep_warm(3)
         vec_bank = matmul_bank([P, P], BF16, "vec_bank")
         nc.tensor.transpose(vec_bank[:], vec_rows[:], ident_b[:])
+        keep_warm(3)
         dist = const.tile([P, 2, 8, 4], F32, name="dist")
         nc.vector.tensor_tensor(
             out=dist[:],
@@ -190,14 +198,17 @@ def tile_gaussianspatialxfeaturelinear_t_kernel(tc, x, cx, cy, sigma, features, 
             if u == 0:
                 nc.vector.reciprocal(out=exp_scale[:], in_=neg_sigma_sq[:])
         spat = const.tile([P, 8, 2, 8], F32, name="spat")
-        feat_bank = matmul_bank([P, 8, C], F32, "feat_bank")
 
-        def build_w(t):
+        def build_w(t, engine="vector"):
             shape = [P, 2, C, 8]
-            in1 = spat[:, t, :, :].unsqueeze(2).to_broadcast(shape)
             dst = w_rows[:, t, :].rearrange("p (u c m) -> p u c m", u=2, c=C)
-            in0 = feat_bank[:, t, :].unsqueeze(1).unsqueeze(3).to_broadcast(shape)
-            nc.vector.tensor_tensor(out=dst, in0=in0, in1=in1, op=ALU.mult)
+            in1 = spat[:, t, :, :].unsqueeze(2).to_broadcast(shape)
+            if engine == "vector":
+                in0 = feat_bank[:, t, :].unsqueeze(1).unsqueeze(3).to_broadcast(shape)
+                nc.vector.tensor_tensor(out=dst, in0=in0, in1=in1, op=ALU.mult)
+            else:
+                in0 = feat[:, t, :].unsqueeze(1).unsqueeze(3).to_broadcast(shape)
+                nc.gpsimd.tensor_tensor(out=dst, in0=in0, in1=in1, op=ALU.mult)
 
         def transpose_w(t):
             bank = transpose_bank([P, 4, P], F32, "tp")
@@ -219,81 +230,100 @@ def tile_gaussianspatialxfeaturelinear_t_kernel(tc, x, cx, cy, sigma, features, 
                     in_=w_bf16[:, g, cols, :].rearrange("p o t -> p (o t)"),
                 )
 
-        nc.tensor.matmul(out=feat_bank[:].rearrange("p t c -> p (t c)"), lhsT=ident_b[:], rhs=feat[:].rearrange("p t c -> p (t c)"), start=True, stop=True)
         bias_bank = matmul_bank([P, O], BF16, "bias_bank")
         for h in range(2):
             half = slice(HALF * h, HALF * h + HALF)
             nc.tensor.matmul(out=bias_bank[:, half], lhsT=ones_b[:], rhs=bias_row[:, half], start=True, stop=True)
-        for t in range(8):
+        feat_bank = matmul_bank([P, 8, C], F32, "feat_bank")
+        nc.tensor.matmul(out=feat_bank[:].rearrange("p t c -> p (t c)"), lhsT=ident_b[:], rhs=feat[:].rearrange("p t c -> p (t c)"), start=True, stop=True)
+        for t in (0, 7, 1, 6, 2, 3, 4, 5):
             nc.scalar.activation(
                 out=spat[:, t, :, :].rearrange("p u m -> p (u m)"),
                 in_=dist_sum[:, t, :, :, :].rearrange("p u i e -> p (u i e)"),
                 func=ACT.Exp,
                 scale=exp_scale[:, t : t + 1],
             )
+        nc.scalar.copy(out=bias_all[:], in_=bias_bank[:])
+        for t in range(4):
+            build_w(t)
+        build_w(7, "gpsimd")
+        build_w(6, "gpsimd")
         transpose_x(0, 0)
         regroup_x(0, 0)
         transpose_x(0, 1)
         regroup_x(0, 1)
-        build_w(0)
-        build_w(1)
+        keep_warm(1)
         transpose_w(0)
+        keep_warm(1)
         transpose_x(0, 2)
         regroup_x(0, 2)
-        build_w(2)
-        build_w(3)
-        nc.vector.tensor_copy(out=bias_all[:], in_=bias_bank[:])
         transpose_w(1)
-        quantise_w(0)
-        quantise_x(0, 0, 2)
+        keep_warm(1)
+        transpose_w(7)
+        keep_warm(1)
         transpose_w(2)
         transpose_x(0, 3)
         regroup_x(0, 3)
+        keep_warm(1)
         transpose_w(3)
-        quantise_w(1)
+        quantise_w(0)
+        quantise_x(0, 0, 2)
+        keep_warm(1)
+        transpose_w(6)
         transpose_x(1, 0)
         regroup_x(1, 0)
-        build_w(4)
-        build_w(5)
-        multiply(0, 0, 0, "scalar")
-        multiply(0, 1, 0, "scalar")
+        quantise_w(1)
         quantise_x(0, 2, 2)
-        build_w(6)
-        transpose_w(4)
-        transpose_w(5)
-        multiply(0, 2, 0, "scalar")
-        multiply(0, 3, 0, "scalar")
-        build_w(7)
-        quantise_w(2)
-        transpose_w(6)
-        transpose_w(7)
-        permute_x(2, 0, 4, "vector")
-        quantise_w(3)
-        quantise_x(1, 0, 1)
-        for r in range(1, TILES):
-            transpose_x(1, r)
+        build_w(4)
         for r in range(TILES):
-            multiply(0, r, 1, "scalar" if r == 0 else "vector")
-            if r > 0:
-                regroup_x(1, r)
-            store(0, r, 1)
-        quantise_x(1, 1, 1)
+            multiply(0, r, 0, "later")
+        transpose_x(1, 1)
+        regroup_x(1, 1)
+        transpose_w(4)
+        build_w(5)
+        quantise_x(1, 0, 2)
+        quantise_w(3)
+        gate = const.tile([P, 1], BF16, name="gate")
+        nc.gpsimd.tensor_copy(out=gate[:], in_=w_rows[:, 5, K - 1 : K])
+        for r in range(TILES):
+            add_bias(0, r, 0)
+        transpose_x(1, 2)
+        regroup_x(1, 2)
+        transpose_w(5)
+        transpose_x(1, 3)
+        regroup_x(1, 3)
+        quantise_w(2)
         quantise_x(1, 2, 2)
+        multiply(1, 0, 0, "vector")
+        multiply(1, 1, 0, "vector")
+        for r in range(TILES):
+            multiply(0, r, 1, "scalar" if r == 3 else "vector")
+            store(0, r, 1)
+        stage_pair(4)
+        multiply(1, 2, 0, "scalar")
+        multiply(1, 3, 0, "vector")
+        quantise_x(2, 0, 2)
+        multiply(1, 0, 1, "vector")
+        store(1, 0, 1)
+        multiply(1, 1, 1, "vector")
+        store(1, 1, 1)
+        stage_pair(5)
+        multiply(1, 2, 1, "scalar")
+        store(1, 2, 1)
+        quantise_x(2, 2, 2)
+        multiply(1, 3, 1, "vector")
+        store(1, 3, 1)
+        stage_pair(6)
 
-        for n in range(1, CHUNKS):
-            ahead = n + 1
-            if ahead < CHUNKS:
-                for r in range(TILES):
-                    transpose_x(ahead, r)
-                for r in range(TILES):
-                    regroup_x(ahead, r)
-            if n + 2 < CHUNKS:
-                permute_x(n + 2, 0, 4, "scalar")
-            for r in range(TILES):
+        for pair in range(4, PAIRS):
+            if pair + 3 < PAIRS:
+                stage_pair(pair + 3)
+            n, first = divmod(pair, 2)
+            for r in (2 * first, 2 * first + 1):
                 for h in range(2):
-                    if ahead < CHUNKS and h == 1 and r in (1, 2):
-                        quantise_x(ahead, 2 * (r - 1), 2)
-                    multiply(n, r, h, "vector")
+                    if (r % 2, h) == (1, 0) and pair + 2 < PAIRS:
+                        quantise_x((pair + 2) // 2, 2 * ((pair + 2) % 2), 2)
+                    multiply(n, r, h, "scalar" if (r % 2, h) == (0, 0) else "vector")
                     if (n, r) == (CHUNKS - 1, TILES - 1):
                         store_half(n, r, h)
                 if (n, r) != (CHUNKS - 1, TILES - 1):

@@ -81,16 +81,28 @@ def tile_gaussianspatialxfeaturelinear_t_kernel(tc, x, cx, cy, sigma, features, 
         x_words = {}
         x_scales = {}
         bias_all = const.tile([P, O], BF16, name="bias_all")
+        x_perm = {}
         x_bf16 = {}
         banks = {}
         y_pairs = {}
 
+        def permute_x(n, r, engine):
+            if n not in x_perm:
+                x_perm[n] = stage.tile([P, TILES, K], BF16, name="xp", bufs=3)
+            dst = x_perm[n][:, r, :].bitcast(F32).rearrange("p (u s i) -> p u s i", u=2, i=8)
+            src = x_raw[n][:, r, :].bitcast(F32).rearrange("p (s u i) -> p u s i", u=2, i=8)
+            if engine == "scalar":
+                nc.scalar.copy(out=dst, in_=src)
+            else:
+                nc.vector.tensor_copy(out=dst, in_=src)
+
         def transpose_x(n, r):
             bank = transpose_bank([P, 4, P], F32, "tp")
+            words = x_perm[n][:, r, :].bitcast(F32)
             for g in range(2):
                 for u in range(2):
-                    words = x_raw[n][:, r, :].bitcast(F32)[:, 2 * P * g + u : 2 * P * (g + 1) : 2]
-                    nc.tensor.transpose(bank[:, 2 * g + u, :], words, ident_f[:])
+                    first = 2 * P * u + P * g
+                    nc.tensor.transpose(bank[:, 2 * g + u, :], words[:, first : first + P], ident_f[:])
             banks[(n, r)] = bank
 
         def regroup_x(n, r, engine="scalar"):
@@ -102,6 +114,11 @@ def tile_gaussianspatialxfeaturelinear_t_kernel(tc, x, cx, cy, sigma, features, 
                 nc.scalar.copy(out=dst, in_=src)
             else:
                 nc.vector.tensor_copy(out=dst, in_=src)
+
+        def permute_pair(pair, engine="scalar"):
+            n, first = divmod(pair, 2)
+            for r in (2 * first, 2 * first + 1):
+                permute_x(n, r, engine)
 
         def stage_pair(pair):
             n, first = divmod(pair, 2)
@@ -186,28 +203,26 @@ def tile_gaussianspatialxfeaturelinear_t_kernel(tc, x, cx, cy, sigma, features, 
         nc.vector.scalar_tensor_tensor(
             out=neg_sigma_sq[:], in0=sigma_col[:], scalar=-1.0, in1=sigma_col[:], op0=ALU.mult, op1=ALU.mult
         )
-        dist_sum = const.tile([P, 8, 2, 4, 2], F32, name="dist_sum")
         exp_scale = const.tile([P, 8], F32, name="exp_scale")
-        for u in range(2):
-            nc.vector.tensor_tensor(
-                out=dist_sum[:, :, u, :, :],
-                in0=dist_sq[:, 0, :, :].unsqueeze(3).to_broadcast([P, 8, 4, 2]),
-                in1=dist_sq[:, 1, :, 2 * u : 2 * u + 2].unsqueeze(2).to_broadcast([P, 8, 4, 2]),
-                op=ALU.add,
-            )
-            if u == 0:
-                nc.vector.reciprocal(out=exp_scale[:], in_=neg_sigma_sq[:])
-        spat = const.tile([P, 8, 2, 8], F32, name="spat")
+        nc.vector.reciprocal(out=exp_scale[:], in_=neg_sigma_sq[:])
+        dist_sum = const.tile([P, 8, 4, 4], F32, name="dist_sum")
+        nc.vector.tensor_tensor(
+            out=dist_sum[:],
+            in0=dist_sq[:, 0, :, :].unsqueeze(3).to_broadcast([P, 8, 4, 4]),
+            in1=dist_sq[:, 1, :, :].unsqueeze(2).to_broadcast([P, 8, 4, 4]),
+            op=ALU.add,
+        )
+        spat = const.tile([P, 8, 16], F32, name="spat")
 
         def build_w(t, engine="vector"):
-            shape = [P, 2, C, 8]
-            dst = w_rows[:, t, :].rearrange("p (u c m) -> p u c m", u=2, c=C)
-            in1 = spat[:, t, :, :].unsqueeze(2).to_broadcast(shape)
+            shape = [P, 2, C // 2, 16]
+            dst = w_rows[:, t, :].rearrange("p (u s m) -> p u s m", u=2, m=16)
+            in1 = spat[:, t, :].unsqueeze(1).unsqueeze(1).to_broadcast(shape)
             if engine == "vector":
-                in0 = feat_bank[:, t, :].unsqueeze(1).unsqueeze(3).to_broadcast(shape)
+                in0 = feat_bank[:, t, :].rearrange("p (s u) -> p u s", u=2).unsqueeze(3).to_broadcast(shape)
                 nc.vector.tensor_tensor(out=dst, in0=in0, in1=in1, op=ALU.mult)
             else:
-                in0 = feat[:, t, :].unsqueeze(1).unsqueeze(3).to_broadcast(shape)
+                in0 = feat[:, t, :].rearrange("p (s u) -> p u s", u=2).unsqueeze(3).to_broadcast(shape)
                 nc.gpsimd.tensor_tensor(out=dst, in0=in0, in1=in1, op=ALU.mult)
 
         def transpose_w(t):
@@ -238,68 +253,78 @@ def tile_gaussianspatialxfeaturelinear_t_kernel(tc, x, cx, cy, sigma, features, 
         nc.tensor.matmul(out=feat_bank[:].rearrange("p t c -> p (t c)"), lhsT=ident_b[:], rhs=feat[:].rearrange("p t c -> p (t c)"), start=True, stop=True)
         for t in (0, 7, 1, 6, 2, 3, 4, 5):
             nc.scalar.activation(
-                out=spat[:, t, :, :].rearrange("p u m -> p (u m)"),
-                in_=dist_sum[:, t, :, :, :].rearrange("p u i e -> p (u i e)"),
+                out=spat[:, t, :],
+                in_=dist_sum[:, t, :, :].rearrange("p i j -> p (i j)"),
                 func=ACT.Exp,
                 scale=exp_scale[:, t : t + 1],
             )
-        nc.scalar.copy(out=bias_all[:], in_=bias_bank[:])
         for t in range(4):
             build_w(t)
         build_w(7, "gpsimd")
         build_w(6, "gpsimd")
+        permute_x(0, 0, "scalar")
+        permute_x(0, 1, "scalar")
         transpose_x(0, 0)
         regroup_x(0, 0)
+        keep_warm(1)
+        transpose_w(0)
         transpose_x(0, 1)
         regroup_x(0, 1)
         keep_warm(1)
-        transpose_w(0)
-        keep_warm(1)
-        transpose_x(0, 2)
-        regroup_x(0, 2)
         transpose_w(1)
-        keep_warm(1)
         transpose_w(7)
         keep_warm(1)
         transpose_w(2)
-        transpose_x(0, 3)
-        regroup_x(0, 3)
+        quantise_w(0)
+        permute_x(0, 2, "vector")
+        permute_x(0, 3, "vector")
+        quantise_x(0, 0, 2)
+        nc.scalar.copy(out=bias_all[:], in_=bias_bank[:])
         keep_warm(1)
         transpose_w(3)
-        quantise_w(0)
-        quantise_x(0, 0, 2)
-        keep_warm(1)
+        transpose_x(0, 2)
+        regroup_x(0, 2)
+        transpose_x(0, 3)
+        regroup_x(0, 3)
+        quantise_w(1)
+        permute_x(1, 0, "vector")
+        permute_x(1, 1, "vector")
+        build_w(4)
+        multiply(0, 0, 0, "later")
+        multiply(0, 1, 0, "later")
         transpose_w(6)
+        quantise_x(0, 2, 2)
+        build_w(5)
         transpose_x(1, 0)
         regroup_x(1, 0)
-        quantise_w(1)
-        quantise_x(0, 2, 2)
-        build_w(4)
-        for r in range(TILES):
-            multiply(0, r, 0, "later")
+        transpose_w(4)
         transpose_x(1, 1)
         regroup_x(1, 1)
-        transpose_w(4)
-        build_w(5)
-        quantise_x(1, 0, 2)
+        multiply(0, 2, 0, "later")
+        multiply(0, 3, 0, "later")
+        permute_x(1, 2, "vector")
+        permute_x(1, 3, "vector")
         quantise_w(3)
         gate = const.tile([P, 1], BF16, name="gate")
         nc.gpsimd.tensor_copy(out=gate[:], in_=w_rows[:, 5, K - 1 : K])
         for r in range(TILES):
             add_bias(0, r, 0)
+        transpose_w(5)
+        quantise_x(1, 0, 2)
         transpose_x(1, 2)
         regroup_x(1, 2)
-        transpose_w(5)
         transpose_x(1, 3)
         regroup_x(1, 3)
         quantise_w(2)
-        quantise_x(1, 2, 2)
         multiply(1, 0, 0, "vector")
-        multiply(1, 1, 0, "vector")
+        multiply(1, 1, 0, "scalar")
+        permute_pair(4)
+        quantise_x(1, 2, 2)
         for r in range(TILES):
-            multiply(0, r, 1, "scalar" if r == 3 else "vector")
+            multiply(0, r, 1, "vector")
             store(0, r, 1)
         stage_pair(4)
+        permute_pair(5)
         multiply(1, 2, 0, "scalar")
         multiply(1, 3, 0, "vector")
         quantise_x(2, 0, 2)
@@ -308,23 +333,25 @@ def tile_gaussianspatialxfeaturelinear_t_kernel(tc, x, cx, cy, sigma, features, 
         multiply(1, 1, 1, "vector")
         store(1, 1, 1)
         stage_pair(5)
+        permute_pair(6)
         multiply(1, 2, 1, "scalar")
         store(1, 2, 1)
         quantise_x(2, 2, 2)
         multiply(1, 3, 1, "vector")
         store(1, 3, 1)
-        stage_pair(6)
 
         for pair in range(4, PAIRS):
-            if pair + 3 < PAIRS:
-                stage_pair(pair + 3)
+            if pair + 2 < PAIRS:
+                stage_pair(pair + 2)
             n, first = divmod(pair, 2)
             for r in (2 * first, 2 * first + 1):
                 for h in range(2):
-                    if (r % 2, h) == (1, 0) and pair + 2 < PAIRS:
+                    if (r % 2, h) == (1, 1) and pair + 2 < PAIRS:
                         quantise_x((pair + 2) // 2, 2 * ((pair + 2) % 2), 2)
                     multiply(n, r, h, "scalar" if (r % 2, h) == (0, 0) else "vector")
                     if (n, r) == (CHUNKS - 1, TILES - 1):
                         store_half(n, r, h)
                 if (n, r) != (CHUNKS - 1, TILES - 1):
                     store(n, r, 1)
+            if pair + 3 < PAIRS:
+                permute_pair(pair + 3)

@@ -115,10 +115,10 @@ def tile_gaussianspatialxfeaturelinear_t_kernel(tc, x, cx, cy, sigma, features, 
             else:
                 nc.vector.tensor_copy(out=dst, in_=src)
 
-        def permute_pair(pair, engine="scalar"):
+        def permute_pair(pair):
             n, first = divmod(pair, 2)
             for r in (2 * first, 2 * first + 1):
-                permute_x(n, r, engine)
+                permute_x(n, r, "scalar" if r % 2 else "vector")
 
         def stage_pair(pair):
             n, first = divmod(pair, 2)
@@ -245,12 +245,12 @@ def tile_gaussianspatialxfeaturelinear_t_kernel(tc, x, cx, cy, sigma, features, 
                     in_=w_bf16[:, g, cols, :].rearrange("p o t -> p (o t)"),
                 )
 
+        feat_bank = matmul_bank([P, 8, C], F32, "feat_bank")
+        nc.tensor.matmul(out=feat_bank[:].rearrange("p t c -> p (t c)"), lhsT=ident_b[:], rhs=feat[:].rearrange("p t c -> p (t c)"), start=True, stop=True)
         bias_bank = matmul_bank([P, O], BF16, "bias_bank")
         for h in range(2):
             half = slice(HALF * h, HALF * h + HALF)
             nc.tensor.matmul(out=bias_bank[:, half], lhsT=ones_b[:], rhs=bias_row[:, half], start=True, stop=True)
-        feat_bank = matmul_bank([P, 8, C], F32, "feat_bank")
-        nc.tensor.matmul(out=feat_bank[:].rearrange("p t c -> p (t c)"), lhsT=ident_b[:], rhs=feat[:].rearrange("p t c -> p (t c)"), start=True, stop=True)
         for t in (0, 7, 1, 6, 2, 3, 4, 5):
             nc.scalar.activation(
                 out=spat[:, t, :],
@@ -258,12 +258,14 @@ def tile_gaussianspatialxfeaturelinear_t_kernel(tc, x, cx, cy, sigma, features, 
                 func=ACT.Exp,
                 scale=exp_scale[:, t : t + 1],
             )
-        for t in range(4):
-            build_w(t)
+        build_w(0)
         build_w(7, "gpsimd")
+        permute_x(0, 0, "vector")
+        permute_x(0, 1, "vector")
+        build_w(1)
         build_w(6, "gpsimd")
-        permute_x(0, 0, "scalar")
-        permute_x(0, 1, "scalar")
+        build_w(2)
+        build_w(3)
         transpose_x(0, 0)
         regroup_x(0, 0)
         keep_warm(1)
@@ -318,8 +320,8 @@ def tile_gaussianspatialxfeaturelinear_t_kernel(tc, x, cx, cy, sigma, features, 
         quantise_w(2)
         multiply(1, 0, 0, "vector")
         multiply(1, 1, 0, "scalar")
-        permute_pair(4)
         quantise_x(1, 2, 2)
+        permute_pair(4)
         for r in range(TILES):
             multiply(0, r, 1, "vector")
             store(0, r, 1)
@@ -343,15 +345,15 @@ def tile_gaussianspatialxfeaturelinear_t_kernel(tc, x, cx, cy, sigma, features, 
         for pair in range(4, PAIRS):
             if pair + 2 < PAIRS:
                 stage_pair(pair + 2)
+            if pair + 3 < PAIRS:
+                permute_pair(pair + 3)
             n, first = divmod(pair, 2)
             for r in (2 * first, 2 * first + 1):
                 for h in range(2):
                     if (r % 2, h) == (1, 1) and pair + 2 < PAIRS:
                         quantise_x((pair + 2) // 2, 2 * ((pair + 2) % 2), 2)
-                    multiply(n, r, h, "scalar" if (r % 2, h) == (0, 0) else "vector")
+                    multiply(n, r, h, "vector")
                     if (n, r) == (CHUNKS - 1, TILES - 1):
                         store_half(n, r, h)
                 if (n, r) != (CHUNKS - 1, TILES - 1):
                     store(n, r, 1)
-            if pair + 3 < PAIRS:
-                permute_pair(pair + 3)

@@ -59,7 +59,6 @@ def tile_gaussianspatialxfeaturelinear_t_kernel(tc, x, cx, cy, sigma, features, 
 
         for n, vec in enumerate((cx, cy, sigma)):
             nc.sync.dma_start(out=vec_rows[8 * n : 8 * n + 8, :], in_=vec.rearrange("(t p) a b c -> t (p a b c)", p=P))
-        nc.sync.dma_start(out=bias_row[0:1, :], in_=bias.rearrange("(a o) -> a o", a=1))
         feat = const.tile([P, 8, C], BF16, name="feat")
         nc.sync.dma_start(out=feat[:], in_=features.rearrange("(t p) c a b -> p t (c a b)", p=P))
         x_raw = []
@@ -69,6 +68,8 @@ def tile_gaussianspatialxfeaturelinear_t_kernel(tc, x, cx, cy, sigma, features, 
             if n < 2:
                 for r in (0, 2):
                     nc.sync.dma_start(out=x_tile[:, r : r + 2, :], in_=x_chunks[n][:, r : r + 2, :])
+                    if (n, r) == (0, 0):
+                        nc.sync.dma_start(out=bias_row[0:1, :], in_=bias.rearrange("(a o) -> a o", a=1))
             else:
                 nc.sync.dma_start(out=x_tile[:], in_=x_chunks[n])
         one_col = const.tile([P, 1], F32, name="one_col")
@@ -184,10 +185,8 @@ def tile_gaussianspatialxfeaturelinear_t_kernel(tc, x, cx, cy, sigma, features, 
         warm_cols = const.tile([P, HALF], BF16, name="warm_cols")
         nc.gpsimd.memset(warm_cols[:], 0.0)
         warm_bank = matmul_bank([P, HALF], F32, "warm_bank")
-        keep_warm(3)
         vec_bank = matmul_bank([P, P], BF16, "vec_bank")
         nc.tensor.transpose(vec_bank[:], vec_rows[:], ident_b[:])
-        keep_warm(3)
         dist = const.tile([P, 2, 8, 4], F32, name="dist")
         nc.vector.tensor_tensor(
             out=dist[:],
@@ -247,10 +246,7 @@ def tile_gaussianspatialxfeaturelinear_t_kernel(tc, x, cx, cy, sigma, features, 
 
         feat_bank = matmul_bank([P, 8, C], F32, "feat_bank")
         nc.tensor.matmul(out=feat_bank[:].rearrange("p t c -> p (t c)"), lhsT=ident_b[:], rhs=feat[:].rearrange("p t c -> p (t c)"), start=True, stop=True)
-        bias_bank = matmul_bank([P, O], BF16, "bias_bank")
-        for h in range(2):
-            half = slice(HALF * h, HALF * h + HALF)
-            nc.tensor.matmul(out=bias_bank[:, half], lhsT=ones_b[:], rhs=bias_row[:, half], start=True, stop=True)
+        keep_warm(3)
         for t in (0, 7, 1, 6, 2, 3, 4, 5):
             nc.scalar.activation(
                 out=spat[:, t, :],
@@ -260,15 +256,18 @@ def tile_gaussianspatialxfeaturelinear_t_kernel(tc, x, cx, cy, sigma, features, 
             )
         build_w(0)
         build_w(7, "gpsimd")
-        permute_x(0, 0, "vector")
-        permute_x(0, 1, "vector")
+        permute_x(0, 0, "scalar")
+        permute_x(0, 1, "scalar")
         build_w(1)
         build_w(6, "gpsimd")
         build_w(2)
         build_w(3)
         transpose_x(0, 0)
         regroup_x(0, 0)
-        keep_warm(1)
+        bias_bank = matmul_bank([P, O], BF16, "bias_bank")
+        for h in range(2):
+            half = slice(HALF * h, HALF * h + HALF)
+            nc.tensor.matmul(out=bias_bank[:, half], lhsT=ones_b[:], rhs=bias_row[:, half], start=True, stop=True)
         transpose_w(0)
         transpose_x(0, 1)
         regroup_x(0, 1)
@@ -324,23 +323,22 @@ def tile_gaussianspatialxfeaturelinear_t_kernel(tc, x, cx, cy, sigma, features, 
         permute_pair(4)
         for r in range(TILES):
             multiply(0, r, 1, "vector")
-            store(0, r, 1)
+            if r % 2 == 1:
+                store(0, r - 1, 2)
         stage_pair(4)
         permute_pair(5)
         multiply(1, 2, 0, "scalar")
         multiply(1, 3, 0, "vector")
         quantise_x(2, 0, 2)
         multiply(1, 0, 1, "vector")
-        store(1, 0, 1)
         multiply(1, 1, 1, "vector")
-        store(1, 1, 1)
+        store(1, 0, 2)
         stage_pair(5)
         permute_pair(6)
         multiply(1, 2, 1, "scalar")
-        store(1, 2, 1)
         quantise_x(2, 2, 2)
         multiply(1, 3, 1, "vector")
-        store(1, 3, 1)
+        store(1, 2, 2)
 
         for pair in range(4, PAIRS):
             if pair + 2 < PAIRS:
@@ -352,8 +350,10 @@ def tile_gaussianspatialxfeaturelinear_t_kernel(tc, x, cx, cy, sigma, features, 
                 for h in range(2):
                     if (r % 2, h) == (1, 1) and pair + 2 < PAIRS:
                         quantise_x((pair + 2) // 2, 2 * ((pair + 2) % 2), 2)
-                    multiply(n, r, h, "vector")
+                    multiply(n, r, h, "scalar" if pair >= PAIRS - 2 and (r % 2, h) == (0, 0) else "vector")
                     if (n, r) == (CHUNKS - 1, TILES - 1):
                         store_half(n, r, h)
-                if (n, r) != (CHUNKS - 1, TILES - 1):
+                if (n, r) == (CHUNKS - 1, TILES - 2):
                     store(n, r, 1)
+                elif r % 2 == 1 and n < CHUNKS - 1 or r == 1:
+                    store(n, r - 1, 2)

@@ -18,7 +18,7 @@ QUARTER = 256
 TILES = 4
 CHUNKS = B // (TILES * P)
 PAIRS = B // (2 * P)
-TRANSPOSE_BANKS = 3
+TRANSPOSE_BANKS = 4
 FLOPS = 2 * B * K * O
 
 
@@ -327,6 +327,7 @@ def tile_gaussianspatialxfeaturelinear_t_kernel(tc, x, cx, cy, sigma, features, 
                 store(0, r - 1, 2)
         stage_pair(4)
         permute_pair(5)
+        permute_pair(6)
         multiply(1, 2, 0, "scalar")
         multiply(1, 3, 0, "vector")
         quantise_x(2, 0, 2)
@@ -334,23 +335,27 @@ def tile_gaussianspatialxfeaturelinear_t_kernel(tc, x, cx, cy, sigma, features, 
         multiply(1, 1, 1, "vector")
         store(1, 0, 2)
         stage_pair(5)
-        permute_pair(6)
+        permute_pair(7)
         multiply(1, 2, 1, "scalar")
         quantise_x(2, 2, 2)
         multiply(1, 3, 1, "vector")
         store(1, 2, 2)
 
-        for pair in range(4, PAIRS):
-            if pair + 2 < PAIRS:
-                stage_pair(pair + 2)
-            if pair + 3 < PAIRS:
-                permute_pair(pair + 3)
-            n, first = divmod(pair, 2)
-            for r in (2 * first, 2 * first + 1):
+
+        for n in range(2, CHUNKS):
+            if n + 1 < CHUNKS:
+                for r in range(TILES):
+                    transpose_x(n + 1, r)
+                for r in range(TILES):
+                    regroup_x(n + 1, r)
+            if n + 2 < CHUNKS:
+                permute_pair(2 * n + 4)
+                permute_pair(2 * n + 5)
+            for r in range(TILES):
                 for h in range(2):
-                    if (r % 2, h) == (1, 1) and pair + 2 < PAIRS:
-                        quantise_x((pair + 2) // 2, 2 * ((pair + 2) % 2), 2)
-                    multiply(n, r, h, "scalar" if pair >= PAIRS - 2 and (r % 2, h) == (0, 0) else "vector")
+                    if h == 1 and r >= 2 and n + 1 < CHUNKS:
+                        quantise_x(n + 1, 2 * r - 4, 2)
+                    multiply(n, r, h, "scalar" if n == CHUNKS - 1 and (r % 2, h) == (0, 0) else "vector")
                     if (n, r) == (CHUNKS - 1, TILES - 1):
                         store_half(n, r, h)
                 if (n, r) == (CHUNKS - 1, TILES - 2):

@@ -44,9 +44,13 @@ def tile_gaussianspatialxfeaturelinear_t_kernel(tc, x, cx, cy, sigma, features, 
         ident_b = const.tile([P, P], BF16, name="ident_b")
         ident_f = const.tile([P, P], F32, name="ident_f")
         make_identity(nc, ident_b[:])
+        warm_cols = const.tile([P, HALF], BF16, name="warm_cols")
+        nc.gpsimd.memset(warm_cols[:], 0.0)
         make_identity(nc, ident_f[:])
         vec_rows = const.tile([P, P], BF16, name="vec_rows")
         nc.vector.memset(vec_rows[:], 0.0)
+        ones_b = const.tile([P, P], BF16, name="ones_b")
+        nc.vector.memset(ones_b[:], 1.0)
         zero_col = const.tile([P, 1], F32, name="zero_col")
         nc.vector.memset(zero_col[:], 0.0)
         grid = const.tile([P, 4], F32, name="grid")
@@ -54,8 +58,6 @@ def tile_gaussianspatialxfeaturelinear_t_kernel(tc, x, cx, cy, sigma, features, 
             nc.vector.memset(grid[:, i : i + 1], i - 1.5)
         bias_row = const.tile([P, O], BF16, name="bias_row")
         nc.vector.memset(bias_row[:], 0.0)
-        ones_b = const.tile([P, P], BF16, name="ones_b")
-        nc.vector.memset(ones_b[:], 1.0)
 
         for n, vec in enumerate((cx, cy, sigma)):
             nc.sync.dma_start(out=vec_rows[8 * n : 8 * n + 8, :], in_=vec.rearrange("(t p) a b c -> t (p a b c)", p=P))
@@ -139,29 +141,37 @@ def tile_gaussianspatialxfeaturelinear_t_kernel(tc, x, cx, cy, sigma, features, 
                 in_=x_bf16[n][:, first : first + count, :].rearrange("p r k -> p (r k)"),
             )
 
-        def multiply(n, r, h, way_out):
+        def multiply(n, r, h, way_out, parts=1):
             if (n, r // 2) not in y_pairs:
                 y_pairs[(n, r // 2)] = outp.tile([P, 2, O], F32, name="y_pair")
-            half = slice(HALF * h, HALF * h + HALF)
+            width = HALF // parts
             bank = matmul_bank([P, HALF], F32, "acc")
-            for g in range(2):
-                cols = slice(2 * P * r + P * g, 2 * P * r + P * g + P)
-                nc.tensor.matmul_mx(
-                    out=bank[:],
-                    lhsT=x_words[n][:, cols].bitcast(FP8X4),
-                    lhsT_scale=x_scales[n][:, cols],
-                    rhs=w_words[:, g, half].bitcast(FP8X4),
-                    rhs_scale=w_scales[:, g, half],
-                    start=(g == 0),
-                    stop=(g == 1),
-                )
-            dst = y_pairs[(n, r // 2)][:, r % 2, half]
-            if way_out == "vector":
-                nc.vector.tensor_tensor(out=dst, in0=bank[:], in1=bias_all[:, half], op=ALU.add)
-            else:
-                nc.scalar.copy(out=dst, in_=bank[:])
-                if way_out == "scalar":
-                    add_bias(n, r, h)
+            for part in range(parts):
+                in_bank = slice(width * part, width * part + width)
+                in_row = slice(HALF * h + width * part, HALF * h + width * part + width)
+                for g in range(2):
+                    cols = slice(2 * P * r + P * g, 2 * P * r + P * g + P)
+                    nc.tensor.matmul_mx(
+                        out=bank[:, in_bank],
+                        lhsT=x_words[n][:, cols].bitcast(FP8X4),
+                        lhsT_scale=x_scales[n][:, cols],
+                        rhs=w_words[:, g, in_row].bitcast(FP8X4),
+                        rhs_scale=w_scales[:, g, in_row],
+                        start=(g == 0),
+                        stop=(g == 1),
+                    )
+            for part in range(parts):
+                in_bank = slice(width * part, width * part + width)
+                in_row = slice(HALF * h + width * part, HALF * h + width * part + width)
+                dst = y_pairs[(n, r // 2)][:, r % 2, in_row]
+                if way_out == "vector":
+                    nc.vector.tensor_tensor(out=dst, in0=bank[:, in_bank], in1=bias_all[:, in_row], op=ALU.add)
+                else:
+                    nc.scalar.copy(out=dst, in_=bank[:, in_bank])
+                    if way_out == "scalar":
+                        add_bias(n, r, h)
+                if parts > 1:
+                    store_columns(n, r, in_row)
 
         def add_bias(n, r, h):
             half = slice(HALF * h, HALF * h + HALF)
@@ -174,19 +184,18 @@ def tile_gaussianspatialxfeaturelinear_t_kernel(tc, x, cx, cy, sigma, features, 
                 in_=y_pairs[(n, first // 2)][:, first % 2 : first % 2 + count, :],
             )
 
-        def store_half(n, r, h):
-            half = slice(HALF * h, HALF * h + HALF)
-            nc.sync.dma_start(out=y_chunks[n][:, r, half], in_=y_pairs[(n, r // 2)][:, r % 2, half])
+        def store_columns(n, r, columns):
+            nc.sync.dma_start(out=y_chunks[n][:, r, columns], in_=y_pairs[(n, r // 2)][:, r % 2, columns])
 
         def keep_warm(count):
             for i in range(count):
                 nc.tensor.matmul(out=warm_bank[:], lhsT=ones_b[:], rhs=warm_cols[:], start=True, stop=True)
 
-        warm_cols = const.tile([P, HALF], BF16, name="warm_cols")
-        nc.gpsimd.memset(warm_cols[:], 0.0)
         warm_bank = matmul_bank([P, HALF], F32, "warm_bank")
         vec_bank = matmul_bank([P, P], BF16, "vec_bank")
+        keep_warm(2)
         nc.tensor.transpose(vec_bank[:], vec_rows[:], ident_b[:])
+        keep_warm(1)
         dist = const.tile([P, 2, 8, 4], F32, name="dist")
         nc.vector.tensor_tensor(
             out=dist[:],
@@ -246,7 +255,7 @@ def tile_gaussianspatialxfeaturelinear_t_kernel(tc, x, cx, cy, sigma, features, 
 
         feat_bank = matmul_bank([P, 8, C], F32, "feat_bank")
         nc.tensor.matmul(out=feat_bank[:].rearrange("p t c -> p (t c)"), lhsT=ident_b[:], rhs=feat[:].rearrange("p t c -> p (t c)"), start=True, stop=True)
-        keep_warm(3)
+        keep_warm(4)
         for t in (0, 7, 1, 6, 2, 3, 4, 5):
             nc.scalar.activation(
                 out=spat[:, t, :],
@@ -283,10 +292,12 @@ def tile_gaussianspatialxfeaturelinear_t_kernel(tc, x, cx, cy, sigma, features, 
         nc.scalar.copy(out=bias_all[:], in_=bias_bank[:])
         keep_warm(1)
         transpose_w(3)
+        keep_warm(1)
         transpose_x(0, 2)
         regroup_x(0, 2)
         transpose_x(0, 3)
         regroup_x(0, 3)
+        keep_warm(2)
         quantise_w(1)
         permute_x(1, 0, "vector")
         permute_x(1, 1, "vector")
@@ -296,8 +307,10 @@ def tile_gaussianspatialxfeaturelinear_t_kernel(tc, x, cx, cy, sigma, features, 
         transpose_w(6)
         quantise_x(0, 2, 2)
         build_w(5)
+        keep_warm(1)
         transpose_x(1, 0)
         regroup_x(1, 0)
+        keep_warm(1)
         transpose_w(4)
         transpose_x(1, 1)
         regroup_x(1, 1)
@@ -355,10 +368,9 @@ def tile_gaussianspatialxfeaturelinear_t_kernel(tc, x, cx, cy, sigma, features, 
                 for h in range(2):
                     if h == 1 and r >= 2 and n + 1 < CHUNKS:
                         quantise_x(n + 1, 2 * r - 4, 2)
-                    multiply(n, r, h, "scalar" if n == CHUNKS - 1 and (r % 2, h) == (0, 0) else "vector")
-                    if (n, r) == (CHUNKS - 1, TILES - 1):
-                        store_half(n, r, h)
-                if (n, r) == (CHUNKS - 1, TILES - 2):
+                    way_out = "scalar" if n == CHUNKS - 1 and (r % 2, h) == (0, 0) else "vector"
+                    multiply(n, r, h, way_out, parts=2 if (n, r) == (CHUNKS - 1, TILES - 1) else 1)
+                if n == CHUNKS - 1 and r < TILES - 1 or n == CHUNKS - 2 and r >= 2:
                     store(n, r, 1)
-                elif r % 2 == 1 and n < CHUNKS - 1 or r == 1:
+                elif n < CHUNKS - 1 and r % 2 == 1:
                     store(n, r - 1, 2)

@@ -121,7 +121,7 @@ def tile_gaussianspatialxfeaturelinear_t_kernel(tc, x, cx, cy, sigma, features, 
         def permute_pair(pair):
             n, first = divmod(pair, 2)
             for r in (2 * first, 2 * first + 1):
-                permute_x(n, r, "scalar" if r % 2 else "vector")
+                permute_x(n, r, "scalar" if n > 3 or r % 2 else "vector")
 
         def stage_pair(pair):
             n, first = divmod(pair, 2)
@@ -145,7 +145,8 @@ def tile_gaussianspatialxfeaturelinear_t_kernel(tc, x, cx, cy, sigma, features, 
             if (n, r // 2) not in y_pairs:
                 y_pairs[(n, r // 2)] = outp.tile([P, 2, O], F32, name="y_pair")
             width = HALF // parts
-            bank = matmul_bank([P, HALF], F32, "acc")
+            new_bank = transpose_bank if n == CHUNKS - 1 and r % 2 == 1 else matmul_bank
+            bank = new_bank([P, HALF], F32, "acc" if new_bank is matmul_bank else "tp")
             for part in range(parts):
                 in_bank = slice(width * part, width * part + width)
                 in_row = slice(HALF * h + width * part, HALF * h + width * part + width)
@@ -186,6 +187,10 @@ def tile_gaussianspatialxfeaturelinear_t_kernel(tc, x, cx, cy, sigma, features, 
 
         def store_columns(n, r, columns):
             nc.sync.dma_start(out=y_chunks[n][:, r, columns], in_=y_pairs[(n, r // 2)][:, r % 2, columns])
+
+        def gpsimd_waits_for(codes):
+            word = stage.tile([P, 1], U32, name="word", bufs=2)
+            nc.gpsimd.tensor_copy(out=word[:], in_=codes)
 
         def keep_warm(count):
             for i in range(count):
@@ -253,6 +258,7 @@ def tile_gaussianspatialxfeaturelinear_t_kernel(tc, x, cx, cy, sigma, features, 
                     in_=w_bf16[:, g, cols, :].rearrange("p o t -> p (o t)"),
                 )
 
+        bias_bank = matmul_bank([P, O], BF16, "bias_bank")
         feat_bank = matmul_bank([P, 8, C], F32, "feat_bank")
         nc.tensor.matmul(out=feat_bank[:].rearrange("p t c -> p (t c)"), lhsT=ident_b[:], rhs=feat[:].rearrange("p t c -> p (t c)"), start=True, stop=True)
         keep_warm(4)
@@ -273,7 +279,6 @@ def tile_gaussianspatialxfeaturelinear_t_kernel(tc, x, cx, cy, sigma, features, 
         build_w(3)
         transpose_x(0, 0)
         regroup_x(0, 0)
-        bias_bank = matmul_bank([P, O], BF16, "bias_bank")
         for h in range(2):
             half = slice(HALF * h, HALF * h + HALF)
             nc.tensor.matmul(out=bias_bank[:, half], lhsT=ones_b[:], rhs=bias_row[:, half], start=True, stop=True)
@@ -299,49 +304,51 @@ def tile_gaussianspatialxfeaturelinear_t_kernel(tc, x, cx, cy, sigma, features, 
         regroup_x(0, 3)
         keep_warm(2)
         quantise_w(1)
-        permute_x(1, 0, "vector")
-        permute_x(1, 1, "vector")
         build_w(4)
+        permute_x(1, 0, "scalar")
         multiply(0, 0, 0, "later")
         multiply(0, 1, 0, "later")
-        transpose_w(6)
         quantise_x(0, 2, 2)
+        transpose_w(6)
         build_w(5)
-        keep_warm(1)
-        transpose_x(1, 0)
-        regroup_x(1, 0)
-        keep_warm(1)
         transpose_w(4)
-        transpose_x(1, 1)
-        regroup_x(1, 1)
-        multiply(0, 2, 0, "later")
-        multiply(0, 3, 0, "later")
+        keep_warm(1)
+        permute_x(1, 1, "vector")
         permute_x(1, 2, "vector")
         permute_x(1, 3, "vector")
+        transpose_x(1, 0)
+        regroup_x(1, 0)
         quantise_w(3)
-        gate = const.tile([P, 1], BF16, name="gate")
-        nc.gpsimd.tensor_copy(out=gate[:], in_=w_rows[:, 5, K - 1 : K])
-        for r in range(TILES):
-            add_bias(0, r, 0)
+        multiply(0, 2, 0, "vector")
+        transpose_x(1, 1)
+        regroup_x(1, 1)
         transpose_w(5)
         quantise_x(1, 0, 2)
+        multiply(0, 3, 0, "vector")
         transpose_x(1, 2)
         regroup_x(1, 2)
         transpose_x(1, 3)
         regroup_x(1, 3)
         quantise_w(2)
+        gpsimd_waits_for(w_words[:, 1, 3 * QUARTER - 1 : 3 * QUARTER])
+        add_bias(0, 0, 0)
         multiply(1, 0, 0, "vector")
-        multiply(1, 1, 0, "scalar")
+        multiply(1, 1, 0, "vector")
         quantise_x(1, 2, 2)
-        permute_pair(4)
+        gpsimd_waits_for(x_words[1][:, TILES * 2 * P - 1 : TILES * 2 * P])
+        add_bias(0, 1, 0)
+        permute_x(2, 0, "scalar")
+        permute_x(2, 1, "scalar")
         for r in range(TILES):
             multiply(0, r, 1, "vector")
             if r % 2 == 1:
                 store(0, r - 1, 2)
+        permute_x(2, 2, "scalar")
+        permute_x(2, 3, "scalar")
         stage_pair(4)
-        permute_pair(5)
-        permute_pair(6)
-        multiply(1, 2, 0, "scalar")
+        permute_x(3, 0, "scalar")
+        permute_x(3, 1, "scalar")
+        multiply(1, 2, 0, "vector")
         multiply(1, 3, 0, "vector")
         quantise_x(2, 0, 2)
         multiply(1, 0, 1, "vector")
@@ -349,7 +356,7 @@ def tile_gaussianspatialxfeaturelinear_t_kernel(tc, x, cx, cy, sigma, features, 
         store(1, 0, 2)
         stage_pair(5)
         permute_pair(7)
-        multiply(1, 2, 1, "scalar")
+        multiply(1, 2, 1, "vector")
         quantise_x(2, 2, 2)
         multiply(1, 3, 1, "vector")
         store(1, 2, 2)
@@ -368,7 +375,7 @@ def tile_gaussianspatialxfeaturelinear_t_kernel(tc, x, cx, cy, sigma, features, 
                 for h in range(2):
                     if h == 1 and r >= 2 and n + 1 < CHUNKS:
                         quantise_x(n + 1, 2 * r - 4, 2)
-                    way_out = "scalar" if n == CHUNKS - 1 and (r % 2, h) == (0, 0) else "vector"
+                    way_out = "scalar" if n == CHUNKS - 1 and (r % 2, h) == (0, 0) or n == CHUNKS - 2 and (r, h) == (2, 0) else "vector"
                     multiply(n, r, h, way_out, parts=2 if (n, r) == (CHUNKS - 1, TILES - 1) else 1)
                 if n == CHUNKS - 1 and r < TILES - 1 or n == CHUNKS - 2 and r >= 2:
                     store(n, r, 1)

from contextlib import ExitStack

import concourse.mybir as mybir
from concourse.masks import make_identity

F32 = mybir.dt.float32
BF16 = mybir.dt.bfloat16
U32 = mybir.dt.uint32
U8 = mybir.dt.uint8
FP8X4 = mybir.dt.float8_e4m3fn_x4
ALU = mybir.AluOpType
ACT = mybir.ActivationFunctionType

P = 128
B, C, O, K = 4096, 64, 1024, 1024
HALF = 512
QUARTER = 256
TILES = 4
CHUNKS = B // (TILES * P)
PAIRS = B // (2 * P)
TRANSPOSE_BANKS = 4
FLOPS = 2 * B * K * O


def tile_gaussianspatialxfeaturelinear_t_kernel(tc, x, cx, cy, sigma, features, bias, out):
    nc = tc.nc
    with ExitStack() as ctx:
        const = ctx.enter_context(tc.tile_pool(name="const", bufs=1))
        xin = ctx.enter_context(tc.tile_pool(name="xin", bufs=1))
        stage = ctx.enter_context(tc.tile_pool(name="stage", bufs=3))
        outp = ctx.enter_context(tc.tile_pool(name="outp", bufs=6))
        psum = ctx.enter_context(tc.psum_pool(name="psum", bufs=4))
        ctx.enter_context(tc.manual_schedule())

        x_chunks = x.rearrange("(n p r) c w h -> n p r (c w h)", p=P, r=TILES)
        y_chunks = out.rearrange("(n p r) o -> n p r o", p=P, r=TILES)

        def transpose_bank(shape, dtype, name):
            return psum.tile(shape, dtype, name=name, tag="tp", bufs=TRANSPOSE_BANKS)

        def matmul_bank(shape, dtype, name):
            return psum.tile(shape, dtype, name=name, tag="acc", bufs=8 - TRANSPOSE_BANKS)

        ident_b = const.tile([P, P], BF16, name="ident_b")
        ident_f = const.tile([P, P], F32, name="ident_f")
        make_identity(nc, ident_b[:])
        warm_cols = const.tile([P, HALF], BF16, name="warm_cols")
        nc.gpsimd.memset(warm_cols[:], 0.0)
        make_identity(nc, ident_f[:])
        vec_rows = const.tile([P, P], BF16, name="vec_rows")
        nc.vector.memset(vec_rows[:], 0.0)
        ones_b = const.tile([P, P], BF16, name="ones_b")
        nc.vector.memset(ones_b[:], 1.0)
        zero_col = const.tile([P, 1], F32, name="zero_col")
        nc.vector.memset(zero_col[:], 0.0)
        grid = const.tile([P, 4], F32, name="grid")
        for i in range(4):
            nc.vector.memset(grid[:, i : i + 1], i - 1.5)
        bias_row = const.tile([P, O], BF16, name="bias_row")
        nc.vector.memset(bias_row[:], 0.0)

        for n, vec in enumerate((cx, cy, sigma)):
            nc.sync.dma_start(out=vec_rows[8 * n : 8 * n + 8, :], in_=vec.rearrange("(t p) a b c -> t (p a b c)", p=P))
        feat = const.tile([P, 8, C], BF16, name="feat")
        nc.sync.dma_start(out=feat[:], in_=features.rearrange("(t p) c a b -> p t (c a b)", p=P))
        x_raw = []
        for n in range(CHUNKS):
            x_tile = xin.tile([P, TILES, K], BF16, name="x%d" % n)
            x_raw.append(x_tile)
            if n < 2:
                for r in (0, 2):
                    nc.sync.dma_start(out=x_tile[:, r : r + 2, :], in_=x_chunks[n][:, r : r + 2, :])
                    if (n, r) == (0, 0):
                        nc.sync.dma_start(out=bias_row[0:1, :], in_=bias.rearrange("(a o) -> a o", a=1))
            else:
                nc.sync.dma_start(out=x_tile[:], in_=x_chunks[n])
        one_col = const.tile([P, 1], F32, name="one_col")
        nc.scalar.activation(out=one_col[:], in_=zero_col[:], func=ACT.Exp)

        w_rows = const.tile([P, 8, K], BF16, name="w_rows")
        w_bf16 = const.tile([P, 2, O, 4], BF16, name="w_bf16", align_bytes=64)
        w_words = const.tile([P, 2, O], U32, name="w_words", align_bytes=64)
        w_scales = const.tile([P, 2, O], U8, name="w_scales", align_bytes=64)
        x_words = {}
        x_scales = {}
        bias_all = const.tile([P, O], BF16, name="bias_all")
        x_perm = {}
        x_bf16 = {}
        banks = {}
        y_pairs = {}

        def permute_x(n, r, engine):
            if n not in x_perm:
                x_perm[n] = stage.tile([P, TILES, K], BF16, name="xp", bufs=3)
            dst = x_perm[n][:, r, :].bitcast(F32).rearrange("p (u s i) -> p u s i", u=2, i=8)
            src = x_raw[n][:, r, :].bitcast(F32).rearrange("p (s u i) -> p u s i", u=2, i=8)
            if engine == "scalar":
                nc.scalar.copy(out=dst, in_=src)
            else:
                nc.vector.tensor_copy(out=dst, in_=src)

        def transpose_x(n, r):
            bank = transpose_bank([P, 4, P], F32, "tp")
            words = x_perm[n][:, r, :].bitcast(F32)
            for g in range(2):
                for u in range(2):
                    first = 2 * P * u + P * g
                    nc.tensor.transpose(bank[:, 2 * g + u, :], words[:, first : first + P], ident_f[:])
            banks[(n, r)] = bank

        def regroup_x(n, r, engine="scalar"):
            if n not in x_bf16:
                x_bf16[n] = stage.tile([P, TILES, K], BF16, name="gx", align_bytes=64)
            dst = x_bf16[n][:, r, :].bitcast(F32).rearrange("p (g b u) -> p g b u", g=2, u=2)
            src = banks[(n, r)][:].rearrange("p (g u) b -> p g b u", g=2)
            if engine == "scalar":
                nc.scalar.copy(out=dst, in_=src)
            else:
                nc.vector.tensor_copy(out=dst, in_=src)

        def permute_pair(pair):
            n, first = divmod(pair, 2)
            for r in (2 * first, 2 * first + 1):
                permute_x(n, r, "scalar" if n > 3 or r % 2 else "vector")

        def stage_pair(pair):
            n, first = divmod(pair, 2)
            for r in (2 * first, 2 * first + 1):
                transpose_x(n, r)
            for r in (2 * first, 2 * first + 1):
                regroup_x(n, r)

        def quantise_x(n, first=0, count=TILES):
            if n not in x_words:
                x_words[n] = stage.tile([P, TILES * 2 * P], U32, name="x_words", bufs=4, align_bytes=64)
                x_scales[n] = stage.tile([P, TILES * 2 * P], U8, name="x_scales", bufs=4, align_bytes=64)
            cols = slice(2 * P * first, 2 * P * (first + count))
            nc.vector.quantize_mx(
                out=x_words[n][:, cols].bitcast(FP8X4),
                scales=x_scales[n][:, cols],
                in_=x_bf16[n][:, first : first + count, :].rearrange("p r k -> p (r k)"),
            )

        def multiply(n, r, h, way_out, parts=1):
            if (n, r // 2) not in y_pairs:
                y_pairs[(n, r // 2)] = outp.tile([P, 2, O], F32, name="y_pair")
            width = HALF // parts
            new_bank = transpose_bank if n == CHUNKS - 1 and r % 2 == 1 else matmul_bank
            bank = new_bank([P, HALF], F32, "acc" if new_bank is matmul_bank else "tp")
            for part in range(parts):
                in_bank = slice(width * part, width * part + width)
                in_row = slice(HALF * h + width * part, HALF * h + width * part + width)
                for g in range(2):
                    cols = slice(2 * P * r + P * g, 2 * P * r + P * g + P)
                    nc.tensor.matmul_mx(
                        out=bank[:, in_bank],
                        lhsT=x_words[n][:, cols].bitcast(FP8X4),
                        lhsT_scale=x_scales[n][:, cols],
                        rhs=w_words[:, g, in_row].bitcast(FP8X4),
                        rhs_scale=w_scales[:, g, in_row],
                        start=(g == 0),
                        stop=(g == 1),
                    )
            for part in range(parts):
                in_bank = slice(width * part, width * part + width)
                in_row = slice(HALF * h + width * part, HALF * h + width * part + width)
                dst = y_pairs[(n, r // 2)][:, r % 2, in_row]
                if way_out == "vector":
                    nc.vector.tensor_tensor(out=dst, in0=bank[:, in_bank], in1=bias_all[:, in_row], op=ALU.add)
                else:
                    nc.scalar.copy(out=dst, in_=bank[:, in_bank])
                    if way_out == "scalar":
                        add_bias(n, r, h)
                if parts > 1:
                    store_columns(n, r, in_row)

        def add_bias(n, r, h):
            half = slice(HALF * h, HALF * h + HALF)
            dst = y_pairs[(n, r // 2)][:, r % 2, half]
            nc.gpsimd.tensor_tensor(out=dst, in0=dst, in1=bias_all[:, half], op=ALU.add)

        def store(n, first, count):
            nc.sync.dma_start(
                out=y_chunks[n][:, first : first + count, :],
                in_=y_pairs[(n, first // 2)][:, first % 2 : first % 2 + count, :],
            )

        def store_columns(n, r, columns):
            nc.sync.dma_start(out=y_chunks[n][:, r, columns], in_=y_pairs[(n, r // 2)][:, r % 2, columns])

        def gpsimd_waits_for(codes):
            word = stage.tile([P, 1], U32, name="word", bufs=2)
            nc.gpsimd.tensor_copy(out=word[:], in_=codes)

        def keep_warm(count):
            for i in range(count):
                nc.tensor.matmul(out=warm_bank[:], lhsT=ones_b[:], rhs=warm_cols[:], start=True, stop=True)

        warm_bank = matmul_bank([P, HALF], F32, "warm_bank")
        vec_bank = matmul_bank([P, P], BF16, "vec_bank")
        keep_warm(2)
        nc.tensor.transpose(vec_bank[:], vec_rows[:], ident_b[:])
        keep_warm(1)
        dist = const.tile([P, 2, 8, 4], F32, name="dist")
        nc.vector.tensor_tensor(
            out=dist[:],
            in0=vec_bank[:, 0:16].rearrange("p (a t) -> p a t", a=2).unsqueeze(3).to_broadcast([P, 2, 8, 4]),
            in1=grid[:].unsqueeze(1).unsqueeze(1).to_broadcast([P, 2, 8, 4]),
            op=ALU.subtract,
        )
        sigma_col = const.tile([P, 8], F32, name="sigma_col")
        nc.vector.tensor_copy(out=sigma_col[:], in_=vec_bank[:, 16:24])
        dist_sq = const.tile([P, 2, 8, 4], F32, name="dist_sq")
        nc.vector.tensor_tensor(out=dist_sq[:], in0=dist[:], in1=dist[:], op=ALU.mult)
        neg_sigma_sq = const.tile([P, 8], F32, name="neg_sigma_sq")
        nc.vector.scalar_tensor_tensor(
            out=neg_sigma_sq[:], in0=sigma_col[:], scalar=-1.0, in1=sigma_col[:], op0=ALU.mult, op1=ALU.mult
        )
        exp_scale = const.tile([P, 8], F32, name="exp_scale")
        nc.vector.reciprocal(out=exp_scale[:], in_=neg_sigma_sq[:])
        dist_sum = const.tile([P, 8, 4, 4], F32, name="dist_sum")
        nc.vector.tensor_tensor(
            out=dist_sum[:],
            in0=dist_sq[:, 0, :, :].unsqueeze(3).to_broadcast([P, 8, 4, 4]),
            in1=dist_sq[:, 1, :, :].unsqueeze(2).to_broadcast([P, 8, 4, 4]),
            op=ALU.add,
        )
        spat = const.tile([P, 8, 16], F32, name="spat")

        def build_w(t, engine="vector"):
            shape = [P, 2, C // 2, 16]
            dst = w_rows[:, t, :].rearrange("p (u s m) -> p u s m", u=2, m=16)
            in1 = spat[:, t, :].unsqueeze(1).unsqueeze(1).to_broadcast(shape)
            if engine == "vector":
                in0 = feat_bank[:, t, :].rearrange("p (s u) -> p u s", u=2).unsqueeze(3).to_broadcast(shape)
                nc.vector.tensor_tensor(out=dst, in0=in0, in1=in1, op=ALU.mult)
            else:
                in0 = feat[:, t, :].rearrange("p (s u) -> p u s", u=2).unsqueeze(3).to_broadcast(shape)
                nc.gpsimd.tensor_tensor(out=dst, in0=in0, in1=in1, op=ALU.mult)

        def transpose_w(t):
            bank = transpose_bank([P, 4, P], F32, "tp")
            for g in range(2):
                for u in range(2):
                    first = 2 * P * u + P * g
                    nc.tensor.transpose(bank[:, 2 * g + u, :], w_rows[:, t, :].bitcast(F32)[:, first : first + P], ident_f[:])
            nc.scalar.copy(
                out=w_bf16[:, :, P * t : P * t + P, :].rearrange("p g o k -> p g (o k)").bitcast(F32).rearrange("p g (o u) -> p g o u", u=2),
                in_=bank[:].rearrange("p (g u) b -> p g b u", g=2),
            )

        def quantise_w(q):
            cols = slice(QUARTER * q, QUARTER * q + QUARTER)
            for g in range(2):
                nc.vector.quantize_mx(
                    out=w_words[:, g, cols].bitcast(FP8X4),
                    scales=w_scales[:, g, cols],
                    in_=w_bf16[:, g, cols, :].rearrange("p o t -> p (o t)"),
                )

        bias_bank = matmul_bank([P, O], BF16, "bias_bank")
        feat_bank = matmul_bank([P, 8, C], F32, "feat_bank")
        nc.tensor.matmul(out=feat_bank[:].rearrange("p t c -> p (t c)"), lhsT=ident_b[:], rhs=feat[:].rearrange("p t c -> p (t c)"), start=True, stop=True)
        keep_warm(4)
        for t in (0, 7, 1, 6, 2, 3, 4, 5):
            nc.scalar.activation(
                out=spat[:, t, :],
                in_=dist_sum[:, t, :, :].rearrange("p i j -> p (i j)"),
                func=ACT.Exp,
                scale=exp_scale[:, t : t + 1],
            )
        build_w(0)
        build_w(7, "gpsimd")
        permute_x(0, 0, "scalar")
        permute_x(0, 1, "scalar")
        build_w(1)
        build_w(6, "gpsimd")
        build_w(2)
        build_w(3)
        transpose_x(0, 0)
        regroup_x(0, 0)
        for h in range(2):
            half = slice(HALF * h, HALF * h + HALF)
            nc.tensor.matmul(out=bias_bank[:, half], lhsT=ones_b[:], rhs=bias_row[:, half], start=True, stop=True)
        transpose_w(0)
        transpose_x(0, 1)
        regroup_x(0, 1)
        keep_warm(1)
        transpose_w(1)
        transpose_w(7)
        keep_warm(1)
        transpose_w(2)
        quantise_w(0)
        permute_x(0, 2, "vector")
        permute_x(0, 3, "vector")
        quantise_x(0, 0, 2)
        nc.scalar.copy(out=bias_all[:], in_=bias_bank[:])
        keep_warm(1)
        transpose_w(3)
        keep_warm(1)
        transpose_x(0, 2)
        regroup_x(0, 2)
        transpose_x(0, 3)
        regroup_x(0, 3)
        keep_warm(2)
        quantise_w(1)
        build_w(4)
        permute_x(1, 0, "scalar")
        multiply(0, 0, 0, "later")
        multiply(0, 1, 0, "later")
        quantise_x(0, 2, 2)
        transpose_w(6)
        build_w(5)
        transpose_w(4)
        keep_warm(1)
        permute_x(1, 1, "vector")
        permute_x(1, 2, "vector")
        permute_x(1, 3, "vector")
        transpose_x(1, 0)
        regroup_x(1, 0)
        quantise_w(3)
        multiply(0, 2, 0, "vector")
        transpose_x(1, 1)
        regroup_x(1, 1)
        transpose_w(5)
        quantise_x(1, 0, 2)
        multiply(0, 3, 0, "vector")
        transpose_x(1, 2)
        regroup_x(1, 2)
        transpose_x(1, 3)
        regroup_x(1, 3)
        quantise_w(2)
        gpsimd_waits_for(w_words[:, 1, 3 * QUARTER - 1 : 3 * QUARTER])
        add_bias(0, 0, 0)
        multiply(1, 0, 0, "vector")
        multiply(1, 1, 0, "vector")
        quantise_x(1, 2, 2)
        gpsimd_waits_for(x_words[1][:, TILES * 2 * P - 1 : TILES * 2 * P])
        add_bias(0, 1, 0)
        permute_x(2, 0, "scalar")
        permute_x(2, 1, "scalar")
        for r in range(TILES):
            multiply(0, r, 1, "vector")
            if r % 2 == 1:
                store(0, r - 1, 2)
        permute_x(2, 2, "scalar")
        permute_x(2, 3, "scalar")
        stage_pair(4)
        permute_x(3, 0, "scalar")
        permute_x(3, 1, "scalar")
        multiply(1, 2, 0, "vector")
        multiply(1, 3, 0, "vector")
        quantise_x(2, 0, 2)
        multiply(1, 0, 1, "vector")
        multiply(1, 1, 1, "vector")
        store(1, 0, 2)
        stage_pair(5)
        permute_pair(7)
        multiply(1, 2, 1, "vector")
        quantise_x(2, 2, 2)
        multiply(1, 3, 1, "vector")
        store(1, 2, 2)


        for n in range(2, CHUNKS):
            if n + 1 < CHUNKS:
                for r in range(TILES):
                    transpose_x(n + 1, r)
                for r in range(TILES):
                    regroup_x(n + 1, r)
            if n + 2 < CHUNKS:
                permute_pair(2 * n + 4)
                permute_pair(2 * n + 5)
            for r in range(TILES):
                for h in range(2):
                    if h == 1 and r >= 2 and n + 1 < CHUNKS:
                        quantise_x(n + 1, 2 * r - 4, 2)
                    way_out = "scalar" if n == CHUNKS - 1 and (r % 2, h) == (0, 0) or n == CHUNKS - 2 and (r, h) == (2, 0) else "vector"
                    multiply(n, r, h, way_out, parts=2 if (n, r) == (CHUNKS - 1, TILES - 1) else 1)
                if n == CHUNKS - 1 and r < TILES - 1 or n == CHUNKS - 2 and r >= 2:
                    store(n, r, 1)
                elif n < CHUNKS - 1 and r % 2 == 1:
                    store(n, r - 1, 2)
